import numpy as np
import ml_dtypes


def mxq(x, axis, fmt="e4m3"):
    dtype, down = {"e4m3": (ml_dtypes.float8_e4m3fn, 7), "e5m2": (ml_dtypes.float8_e5m2, 14)}[fmt]
    v = np.moveaxis(np.asarray(x, np.float32).astype(ml_dtypes.bfloat16).astype(np.float64), axis, -1)
    blocks = v.reshape(v.shape[:-1] + (-1, 32))
    amax = np.abs(blocks).max(-1, keepdims=True)
    byte = np.maximum(np.where(amax > 0, np.frexp(amax)[1] - 1 + 127, 0) - down, 1)
    scale = np.exp2(byte - 127.0)
    codes = (blocks / scale).astype(np.float32).astype(dtype).astype(np.float64)
    return np.moveaxis((codes * scale).reshape(v.shape), -1, axis)


WIDE = False


def mx_kscale(k):
    if not WIDE:
        return np.ones(k)
    levels = np.array([10, -10, 5, -5, 0])
    a = np.random.permutation(np.resize(levels, k // 512 * 4)).reshape(k // 512, 4)
    idx = np.arange(k)
    return np.exp2(a[idx // 512, idx % 128 // 32])


BF16 = ml_dtypes.bfloat16


def bf(x):
    return np.asarray(x, np.float32).astype(BF16)


def f64(x):
    return np.asarray(x).astype(np.float64)


B, C, RR, O, H, W = 8, 512, 16, 128, 32, 32
N = H * W
E0 = 7.0
YS = np.sqrt(E0 / N)
PEAK = 1.8


def setup_inputs():
    u = mx_kscale(C + C)
    t, s = u[:C], u[C:]
    logits = PEAK * np.random.standard_normal((B, C, C))
    p = np.exp(logits - logits.max(-1, keepdims=True))
    attention = p / p.sum(-1, keepdims=True)
    wz = np.random.standard_normal((O, C)) * 0.6 / (YS * np.sqrt(C)) / t
    wx = np.random.standard_normal((O, C)) * 0.7 / np.sqrt(C) / s
    return {"attention": bf(attention * t[:, None] / t[None, :]),
            "v": bf(YS * np.random.standard_normal((B, C, N)) * t[:, None]),
            "x": bf(np.random.standard_normal((B, C, N)) * s[:, None]),
            "wf": bf(np.concatenate([wz, wx], axis=1)),
            "b_fuse": bf(0.2 * np.random.standard_normal(O)),
            "gamma": bf(2.0 + 0.2 * np.random.standard_normal(1))}


def reference(attention, v, x, wf, b_fuse, gamma):
    v = f64(v)
    mixed = mxq(f64(attention), 2, "e4m3") @ mxq(v, 1, "e4m3")
    z = f64(gamma) * mixed + v
    cat = np.concatenate([z, f64(x)], axis=1)
    fused = mxq(f64(wf), 1, "e4m3") @ mxq(cat, 1, "e4m3")
    return fused + f64(b_fuse)[None, :, None]

@@ -1,0 +1,281 @@
+from contextlib import ExitStack
+
+import concourse.mybir as mybir
+from concourse.masks import make_identity
+
+BF16 = mybir.dt.bfloat16
+F32 = mybir.dt.float32
+U32 = mybir.dt.uint32
+U8 = mybir.dt.uint8
+FP8X4 = mybir.dt.float8_e4m3fn_x4
+ALU = mybir.AluOpType
+ACT = mybir.ActivationFunctionType
+
+B, C, N, O = 8, 512, 1024, 128
+P = 128
+PACK = 4
+NB = 128
+NH = 512
+XV = 256
+RAW_BUFS = 4
+FLOPS = 2 * B * C * C * N + 2 * B * O * 2 * C * N
+
+
+def tile_gcam_pb_t_kernel(tc, attention, v, x, wf, b_fuse, gamma, out):
+    nc = tc.nc
+    with ExitStack() as ctx:
+        consts = ctx.enter_context(tc.tile_pool(name="consts", bufs=1))
+        raw = ctx.enter_context(tc.tile_pool(name="raw", bufs=RAW_BUFS))
+        grp = ctx.enter_context(tc.tile_pool(name="grp", bufs=2))
+        cod = ctx.enter_context(tc.tile_pool(name="cod", bufs=2))
+        res = ctx.enter_context(tc.tile_pool(name="res", bufs=2))
+        ps_t = ctx.enter_context(tc.psum_pool(name="ps_t", bufs=2))
+        ps_a = ctx.enter_context(tc.psum_pool(name="ps_a", bufs=4))
+        ps_o = ctx.enter_context(tc.psum_pool(name="ps_o", bufs=2))
+        ctx.enter_context(tc.manual_schedule())
+
+        st = {}
+        for b in range(B):
+            st[b] = {}
+
+        def regroup(engine_copy, dst, src, lo, hi):
+            engine_copy(
+                out=dst[:, lo:hi, :].rearrange("p (c i) t -> p c t i", i=4),
+                in_=src[:, :, lo:hi].rearrange("p t (c i) -> p c t i", i=4),
+            )
+
+        def quantise(codes, scales, grouped, lo, hi):
+            nc.vector.quantize_mx(
+                out=codes[:, lo:hi].bitcast(FP8X4),
+                scales=scales[:, lo:hi],
+                in_=grouped[:, lo:hi, :].rearrange("p n t -> p (n t)"),
+            )
+
+        def transpose_words(words, dst_words, col0):
+            tp = ps_t.tile([P, 2, 256], F32, name="tp", tag="tp")
+            for blk in range(2):
+                for u in range(2):
+                    nc.tensor.transpose(
+                        tp[:, u, blk * P : (blk + 1) * P], words[:, blk, u, :], ident[:]
+                    )
+            nc.scalar.copy(
+                out=dst_words[:, col0 : col0 + 256, :],
+                in_=tp[:].rearrange("p u c -> p c u"),
+            )
+
+        def load_att(b):
+            if b >= B:
+                return
+            t = raw.tile([P, PACK, C], BF16, name="att_raw", tag="att_raw")
+            nc.sync.dma_start(out=t[:], in_=attention[b].rearrange("(p t) d -> p t d", t=PACK))
+            st[b]["att_raw"] = t
+
+        def load_big(b, key, src, pieces):
+            if b >= B:
+                return
+            t = raw.tile([P, PACK, N], BF16, name=key, tag=key)
+            view = src[b].rearrange("(p t) n -> p t n", t=PACK)
+            w = N // pieces
+            for k in range(pieces):
+                nc.sync.dma_start(out=t[:, :, k * w : (k + 1) * w], in_=view[:, :, k * w : (k + 1) * w])
+            st[b][key] = t
+
+        def alloc_v(b):
+            s = st[b]
+            s["vg"] = grp.tile([P, N, PACK], BF16, name="vg", tag="vg", align_bytes=64)
+            s["v_codes"] = cod.tile([P, N], U32, name="v_codes", tag="v_codes", align_bytes=64)
+            s["v_scales"] = cod.tile([P, N], U8, name="v_scales", tag="v_scales", align_bytes=64)
+
+        def alloc_x(b):
+            s = st[b]
+            s["xg"] = grp.tile([P, N, PACK], BF16, name="xg", tag="xg", align_bytes=64)
+            s["x_codes"] = cod.tile([P, N], U32, name="x_codes", tag="x_codes", align_bytes=64)
+            s["x_scales"] = cod.tile([P, N], U8, name="x_scales", tag="x_scales", align_bytes=64)
+
+        def t_sa(b):
+            s = st[b]
+            s["attg"] = grp.tile([P, C, PACK], BF16, name="attg", tag="attg", align_bytes=64)
+            words = s["att_raw"][:].bitcast(F32).rearrange("p t (i u) -> p t u i", u=2)
+            for h in range(2):
+                transpose_words(words[:, 2 * h : 2 * h + 2, :, :], s["attg"][:].bitcast(F32), 256 * h)
+
+        def qa(b):
+            s = st[b]
+            s["att_codes"] = cod.tile([P, C], U32, name="att_codes", tag="att_codes", align_bytes=64)
+            s["att_scales"] = cod.tile([P, C], U8, name="att_scales", tag="att_scales", align_bytes=64)
+            quantise(s["att_codes"], s["att_scales"], s["attg"], 0, C)
+
+        def qv(b, h):
+            s = st[b]
+            quantise(s["v_codes"], s["v_scales"], s["vg"], h * NH, (h + 1) * NH)
+
+        def qx(b, h):
+            s = st[b]
+            quantise(s["x_codes"], s["x_scales"], s["xg"], h * NH, (h + 1) * NH)
+
+        def m1(b, nb):
+            s = st[b]
+            cols = slice(nb * NB, (nb + 1) * NB)
+            acc = ps_a.tile([P, PACK, NB], F32, name="acc", tag="acc")
+            for t in range(PACK):
+                rows = slice(t * P, (t + 1) * P)
+                nc.tensor.matmul_mx(
+                    out=acc[:, t, :],
+                    lhsT=s["att_codes"][:, rows].bitcast(FP8X4),
+                    lhsT_scale=s["att_scales"][:, rows],
+                    rhs=s["v_codes"][:, cols].bitcast(FP8X4),
+                    rhs_scale=s["v_scales"][:, cols],
+                    start=True,
+                    stop=True,
+                )
+            s["acc", nb] = acc
+
+        def stt(b, nb):
+            s = st[b]
+            cols = slice(nb * NB, (nb + 1) * NB)
+            nc.vector.scalar_tensor_tensor(
+                out=s["zg"][:, cols, :],
+                in0=s["acc", nb][:].rearrange("p t n -> p n t"),
+                scalar=gamma_f[:, 0:1],
+                in1=s["vg"][:, cols, :],
+                op0=ALU.mult,
+                op1=ALU.add,
+            )
+
+        def qz(b, h):
+            s = st[b]
+            quantise(s["z_codes"], s["z_scales"], s["zg"], h * NH, (h + 1) * NH)
+
+        def m2(b, h):
+            s = st[b]
+            cols = slice(h * NH, (h + 1) * NH)
+            acc2 = ps_o.tile([P, NH], F32, name="acc2", tag="acc2")
+            nc.tensor.matmul_mx(
+                out=acc2[:],
+                lhsT=wf_codes[:, P : 2 * P].bitcast(FP8X4),
+                lhsT_scale=wf_scales[:, P : 2 * P],
+                rhs=s["x_codes"][:, cols].bitcast(FP8X4),
+                rhs_scale=s["x_scales"][:, cols],
+                start=True,
+                stop=False,
+            )
+            nc.tensor.matmul_mx(
+                out=acc2[:],
+                lhsT=wf_codes[:, 0:P].bitcast(FP8X4),
+                lhsT_scale=wf_scales[:, 0:P],
+                rhs=s["z_codes"][:, cols].bitcast(FP8X4),
+                rhs_scale=s["z_scales"][:, cols],
+                start=False,
+                stop=True,
+            )
+            s["acc2", h] = acc2
+
+        def so(b, h):
+            s = st[b]
+            cols = slice(h * NH, (h + 1) * NH)
+            nc.scalar.activation(
+                out=s["out_sb"][:, cols], in_=s["acc2", h][:], func=ACT.Identity,
+                bias=bias_f[:, 0:1], scale=1.0,
+            )
+
+        def period(i):
+            nxt = i + 1
+            more = nxt < B
+            s = st[i]
+            if more:
+                alloc_v(nxt)
+                regroup(nc.scalar.copy, st[nxt]["vg"], st[nxt]["v_raw"], 0, NH)
+                regroup(nc.scalar.copy, st[nxt]["vg"], st[nxt]["v_raw"], NH, N)
+                load_big(nxt + RAW_BUFS, "v_raw", v, 1)
+            s["zg"] = grp.tile([P, N, PACK], BF16, name="zg", tag="zg", align_bytes=64)
+            s["z_codes"] = cod.tile([P, N], U32, name="z_codes", tag="z_codes", align_bytes=64)
+            s["z_scales"] = cod.tile([P, N], U8, name="z_scales", tag="z_scales", align_bytes=64)
+            s["out_sb"] = res.tile([P, N], F32, name="out_sb", tag="out_sb")
+            for nb in range(4):
+                m1(i, nb)
+            if more:
+                t_sa(nxt)
+                load_att(nxt + RAW_BUFS)
+            if i == 0:
+                stt(i, 0)
+                stt(i, 1)
+                stt(i, 2)
+                qv(i, 1)
+                for nb in range(3, 8):
+                    if nb + 1 < 8:
+                        m1(i, nb + 1)
+                    stt(i, nb)
+            else:
+                for nb in range(8):
+                    stt(i, nb)
+                    if nb + 4 < 8:
+                        m1(i, nb + 4)
+            if more:
+                alloc_x(nxt)
+                regroup(nc.scalar.copy, st[nxt]["xg"], st[nxt]["x_raw"], 0, NH)
+                regroup(nc.scalar.copy, st[nxt]["xg"], st[nxt]["x_raw"], NH, N - XV)
+            for h in range(2):
+                qx(i, h)
+                qz(i, h)
+                m2(i, h)
+            if more:
+                regroup(nc.vector.tensor_copy, st[nxt]["xg"], st[nxt]["x_raw"], N - XV, N)
+                load_big(nxt + RAW_BUFS, "x_raw", x, 1)
+            for h in range(2):
+                so(i, h)
+                if not more:
+                    cols = slice(h * NH, (h + 1) * NH)
+                    nc.sync.dma_start(out=out[i][:, cols], in_=s["out_sb"][:, cols])
+            if more:
+                nc.sync.dma_start(out=out[i], in_=s["out_sb"][:])
+                qv(nxt, 0)
+                qa(nxt)
+                qv(nxt, 1)
+
+        gamma_b = consts.tile([P, 1], BF16, name="gamma_b")
+        nc.scalar.dma_start(out=gamma_b[:], in_=gamma.partition_broadcast(P))
+        bias_b = consts.tile([P, 1], BF16, name="bias_b")
+        with nc.allow_non_contiguous_dma(reason="one bias value a partition, 128 in all"):
+            nc.scalar.dma_start(out=bias_b[:], in_=b_fuse.rearrange("(o one) -> o one", one=1))
+        wf_raw = consts.tile([P, 2 * C], BF16, name="wf_raw")
+        load_att(0)
+        load_big(0, "v_raw", v, 2)
+        nc.scalar.dma_start(out=wf_raw[:], in_=wf)
+        load_big(0, "x_raw", x, 1)
+        for b in range(1, RAW_BUFS):
+            load_big(b, "v_raw", v, 1)
+            load_att(b)
+            load_big(b, "x_raw", x, 1)
+
+        ident = consts.tile([P, P], F32, name="ident")
+        make_identity(nc, ident[:])
+        gamma_f = consts.tile([P, 1], F32, name="gamma_f")
+        nc.vector.tensor_copy(out=gamma_f[:], in_=gamma_b[:])
+        bias_f = consts.tile([P, 1], F32, name="bias_f")
+        nc.vector.tensor_copy(out=bias_f[:], in_=bias_b[:])
+
+        t_sa(0)
+        load_att(RAW_BUFS)
+        wfg = consts.tile([P, 2 * O, PACK], BF16, name="wfg", align_bytes=64)
+        wf_codes = consts.tile([P, 2 * O], U32, name="wf_codes", align_bytes=64)
+        wf_scales = consts.tile([P, 2 * O], U8, name="wf_scales", align_bytes=64)
+        transpose_words(
+            wf_raw[:].bitcast(F32).rearrange("p (g i u) -> p g u i", g=2, u=2),
+            wfg[:].bitcast(F32),
+            0,
+        )
+        alloc_v(0)
+        regroup(nc.vector.tensor_copy, st[0]["vg"], st[0]["v_raw"], 0, 256)
+        regroup(nc.vector.tensor_copy, st[0]["vg"], st[0]["v_raw"], 256, NH)
+        regroup(nc.scalar.copy, st[0]["vg"], st[0]["v_raw"], NH, N)
+        load_big(RAW_BUFS, "v_raw", v, 1)
+        qv(0, 0)
+        qa(0)
+        quantise(wf_codes, wf_scales, wfg, 0, 2 * O)
+        alloc_x(0)
+        regroup(nc.scalar.copy, st[0]["xg"], st[0]["x_raw"], 0, NH)
+        regroup(nc.scalar.copy, st[0]["xg"], st[0]["x_raw"], NH, N)
+        load_big(RAW_BUFS, "x_raw", x, 1)
+
+        for i in range(B):
+            period(i)

@@ -16,7 +16,9 @@ P = 128
 PACK = 4
 NB = 128
 NH = 512
-XV = 256
+XG = 512
+XS = N - XG
+GW = 128
 RAW_BUFS = 4
 FLOPS = 2 * B * C * C * N + 2 * B * O * 2 * C * N
 
@@ -88,7 +90,7 @@ def tile_gcam_pb_t_kernel(tc, attention, v, x, wf, b_fuse, gamma, out):
 
         def alloc_x(b):
             s = st[b]
-            s["xg"] = grp.tile([P, N, PACK], BF16, name="xg", tag="xg", align_bytes=64)
+            s["xg"] = grp.tile([P, XS, PACK], BF16, name="xg", tag="xg", align_bytes=64)
             s["x_codes"] = cod.tile([P, N], U32, name="x_codes", tag="x_codes", align_bytes=64)
             s["x_scales"] = cod.tile([P, N], U8, name="x_scales", tag="x_scales", align_bytes=64)
 
@@ -109,9 +111,33 @@ def tile_gcam_pb_t_kernel(tc, attention, v, x, wf, b_fuse, gamma, out):
             s = st[b]
             quantise(s["v_codes"], s["v_scales"], s["vg"], h * NH, (h + 1) * NH)
 
-        def qx(b, h):
+        def qxs(b):
             s = st[b]
-            quantise(s["x_codes"], s["x_scales"], s["xg"], h * NH, (h + 1) * NH)
+            quantise(s["x_codes"], s["x_scales"], s["xg"], 0, XS)
+
+        def qxg(b):
+            s = st[b]
+            nc.vector.quantize_mx(
+                out=s["x_codes"][:, XS:N].bitcast(FP8X4),
+                scales=s["x_scales"][:, XS:N],
+                in_=s["xgg"][:].rearrange("p n t -> p (n t)"),
+            )
+
+        def tick_gx(b):
+            s = st[b]
+            tick = grp.tile([P, 1], F32, name="tick", tag="tick")
+            nc.vector.memset(tick[:], 1.0)
+            s["xgg"] = grp.tile([P, XG, PACK], BF16, name="xgg", tag="xgg", align_bytes=64)
+            for lo in range(0, XG, GW):
+                nc.gpsimd.tensor_scalar(
+                    out=s["xgg"][:, lo : lo + GW, :],
+                    in0=s["x_raw"][:, :, XS + lo : XS + lo + GW].rearrange("p t n -> p n t"),
+                    scalar1=tick[:, 0:1],
+                    scalar2=0.0,
+                    op0=ALU.mult,
+                    op1=ALU.add,
+                )
+            load_big(b + RAW_BUFS, "x_raw", x, 1)
 
         def m1(b, nb):
             s = st[b]
@@ -191,6 +217,7 @@ def tile_gcam_pb_t_kernel(tc, attention, v, x, wf, b_fuse, gamma, out):
             s["z_codes"] = cod.tile([P, N], U32, name="z_codes", tag="z_codes", align_bytes=64)
             s["z_scales"] = cod.tile([P, N], U8, name="z_scales", tag="z_scales", align_bytes=64)
             s["out_sb"] = res.tile([P, N], F32, name="out_sb", tag="out_sb")
+            tick_gx(i)
             for nb in range(4):
                 m1(i, nb)
             if more:
@@ -212,15 +239,13 @@ def tile_gcam_pb_t_kernel(tc, attention, v, x, wf, b_fuse, gamma, out):
                         m1(i, nb + 4)
             if more:
                 alloc_x(nxt)
-                regroup(nc.scalar.copy, st[nxt]["xg"], st[nxt]["x_raw"], 0, NH)
-                regroup(nc.scalar.copy, st[nxt]["xg"], st[nxt]["x_raw"], NH, N - XV)
-            for h in range(2):
-                qx(i, h)
-                qz(i, h)
-                m2(i, h)
-            if more:
-                regroup(nc.vector.tensor_copy, st[nxt]["xg"], st[nxt]["x_raw"], N - XV, N)
-                load_big(nxt + RAW_BUFS, "x_raw", x, 1)
+                regroup(nc.scalar.copy, st[nxt]["xg"], st[nxt]["x_raw"], 0, XS)
+            qxs(i)
+            qz(i, 0)
+            m2(i, 0)
+            qz(i, 1)
+            qxg(i)
+            m2(i, 1)
             for h in range(2):
                 so(i, h)
                 if not more:
@@ -273,9 +298,7 @@ def tile_gcam_pb_t_kernel(tc, attention, v, x, wf, b_fuse, gamma, out):
         qa(0)
         quantise(wf_codes, wf_scales, wfg, 0, 2 * O)
         alloc_x(0)
-        regroup(nc.scalar.copy, st[0]["xg"], st[0]["x_raw"], 0, NH)
-        regroup(nc.scalar.copy, st[0]["xg"], st[0]["x_raw"], NH, N)
-        load_big(RAW_BUFS, "x_raw", x, 1)
+        regroup(nc.scalar.copy, st[0]["xg"], st[0]["x_raw"], 0, XS)
 
         for i in range(B):
             period(i)

@@ -16,6 +16,7 @@ P = 128
 PACK = 4
 NB = 128
 NH = 512
+NQ = 256
 XG = 512
 XS = N - XG
 GW = 128
@@ -30,7 +31,7 @@ def tile_gcam_pb_t_kernel(tc, attention, v, x, wf, b_fuse, gamma, out):
         raw = ctx.enter_context(tc.tile_pool(name="raw", bufs=RAW_BUFS))
         grp = ctx.enter_context(tc.tile_pool(name="grp", bufs=2))
         cod = ctx.enter_context(tc.tile_pool(name="cod", bufs=2))
-        res = ctx.enter_context(tc.tile_pool(name="res", bufs=2))
+        res = ctx.enter_context(tc.tile_pool(name="res", bufs=4))
         ps_t = ctx.enter_context(tc.psum_pool(name="ps_t", bufs=2))
         ps_a = ctx.enter_context(tc.psum_pool(name="ps_a", bufs=4))
         ps_o = ctx.enter_context(tc.psum_pool(name="ps_o", bufs=2))
@@ -40,17 +41,17 @@ def tile_gcam_pb_t_kernel(tc, attention, v, x, wf, b_fuse, gamma, out):
         for b in range(B):
             st[b] = {}
 
-        def regroup(engine_copy, dst, src, lo, hi):
+        def regroup(engine_copy, dst, src, lo, hi, dst_lo):
             engine_copy(
-                out=dst[:, lo:hi, :].rearrange("p (c i) t -> p c t i", i=4),
+                out=dst[:, dst_lo : dst_lo + hi - lo, :].rearrange("p (c i) t -> p c t i", i=4),
                 in_=src[:, :, lo:hi].rearrange("p t (c i) -> p c t i", i=4),
             )
 
-        def quantise(codes, scales, grouped, lo, hi):
+        def quantise(codes, scales, grouped, lo, hi, src_lo):
             nc.vector.quantize_mx(
                 out=codes[:, lo:hi].bitcast(FP8X4),
                 scales=scales[:, lo:hi],
-                in_=grouped[:, lo:hi, :].rearrange("p n t -> p (n t)"),
+                in_=grouped[:, src_lo : src_lo + hi - lo, :].rearrange("p n t -> p (n t)"),
             )
 
         def transpose_words(words, dst_words, col0):
@@ -65,22 +66,33 @@ def tile_gcam_pb_t_kernel(tc, attention, v, x, wf, b_fuse, gamma, out):
                 in_=tp[:].rearrange("p u c -> p c u"),
             )
 
-        def load_att(b):
+        def load_att(b, pieces):
             if b >= B:
                 return
             t = raw.tile([P, PACK, C], BF16, name="att_raw", tag="att_raw")
-            nc.sync.dma_start(out=t[:], in_=attention[b].rearrange("(p t) d -> p t d", t=PACK))
+            view = attention[b].rearrange("(p t) d -> p t d", t=PACK)
+            w = PACK // pieces
+            for k in range(pieces):
+                nc.sync.dma_start(out=t[:, k * w : (k + 1) * w, :], in_=view[:, k * w : (k + 1) * w, :])
             st[b]["att_raw"] = t
 
-        def load_big(b, key, src, pieces):
+        def load_v(b, pieces):
             if b >= B:
                 return
-            t = raw.tile([P, PACK, N], BF16, name=key, tag=key)
-            view = src[b].rearrange("(p t) n -> p t n", t=PACK)
+            t = raw.tile([P, PACK, N], BF16, name="v_raw", tag="v_raw")
+            view = v[b].rearrange("(p t) n -> p t n", t=PACK)
             w = N // pieces
             for k in range(pieces):
                 nc.sync.dma_start(out=t[:, :, k * w : (k + 1) * w], in_=view[:, :, k * w : (k + 1) * w])
-            st[b][key] = t
+            st[b]["v_raw"] = t
+
+        def load_x(b, lo, hi):
+            if b >= B:
+                return
+            if "x_raw" not in st[b]:
+                st[b]["x_raw"] = raw.tile([P, PACK, N], BF16, name="x_raw", tag="x_raw")
+            view = x[b].rearrange("(p t) n -> p t n", t=PACK)
+            nc.sync.dma_start(out=st[b]["x_raw"][:, :, lo:hi], in_=view[:, :, lo:hi])
 
         def alloc_v(b):
             s = st[b]
@@ -88,11 +100,18 @@ def tile_gcam_pb_t_kernel(tc, attention, v, x, wf, b_fuse, gamma, out):
             s["v_codes"] = cod.tile([P, N], U32, name="v_codes", tag="v_codes", align_bytes=64)
             s["v_scales"] = cod.tile([P, N], U8, name="v_scales", tag="v_scales", align_bytes=64)
 
-        def alloc_x(b):
+        def rv(engine_copy, b, lo, hi):
+            regroup(engine_copy, st[b]["vg"], st[b]["v_raw"], lo, hi, lo)
+
+        def alloc_xc(b):
             s = st[b]
-            s["xg"] = grp.tile([P, XS, PACK], BF16, name="xg", tag="xg", align_bytes=64)
             s["x_codes"] = cod.tile([P, N], U32, name="x_codes", tag="x_codes", align_bytes=64)
             s["x_scales"] = cod.tile([P, N], U8, name="x_scales", tag="x_scales", align_bytes=64)
+
+        def sxs(b):
+            s = st[b]
+            s["xg"] = grp.tile([P, XS, PACK], BF16, name="xg", tag="xg", align_bytes=64)
+            regroup(nc.scalar.copy, s["xg"], s["x_raw"], 0, XS, 0)
 
         def t_sa(b):
             s = st[b]
@@ -101,27 +120,26 @@ def tile_gcam_pb_t_kernel(tc, attention, v, x, wf, b_fuse, gamma, out):
             for h in range(2):
                 transpose_words(words[:, 2 * h : 2 * h + 2, :, :], s["attg"][:].bitcast(F32), 256 * h)
 
-        def qa(b):
+        def alloc_ac(b):
             s = st[b]
             s["att_codes"] = cod.tile([P, C], U32, name="att_codes", tag="att_codes", align_bytes=64)
             s["att_scales"] = cod.tile([P, C], U8, name="att_scales", tag="att_scales", align_bytes=64)
-            quantise(s["att_codes"], s["att_scales"], s["attg"], 0, C)
 
-        def qv(b, h):
+        def qa(b, lo, hi):
             s = st[b]
-            quantise(s["v_codes"], s["v_scales"], s["vg"], h * NH, (h + 1) * NH)
+            quantise(s["att_codes"], s["att_scales"], s["attg"], lo, hi, lo)
+
+        def qv(b, lo, hi):
+            s = st[b]
+            quantise(s["v_codes"], s["v_scales"], s["vg"], lo, hi, lo)
 
         def qxs(b):
             s = st[b]
-            quantise(s["x_codes"], s["x_scales"], s["xg"], 0, XS)
+            quantise(s["x_codes"], s["x_scales"], s["xg"], 0, XS, 0)
 
         def qxg(b):
             s = st[b]
-            nc.vector.quantize_mx(
-                out=s["x_codes"][:, XS:N].bitcast(FP8X4),
-                scales=s["x_scales"][:, XS:N],
-                in_=s["xgg"][:].rearrange("p n t -> p (n t)"),
-            )
+            quantise(s["x_codes"], s["x_scales"], s["xgg"], XS, N, 0)
 
         def tick_gx(b):
             s = st[b]
@@ -137,7 +155,12 @@ def tile_gcam_pb_t_kernel(tc, attention, v, x, wf, b_fuse, gamma, out):
                     op0=ALU.mult,
                     op1=ALU.add,
                 )
-            load_big(b + RAW_BUFS, "x_raw", x, 1)
+
+        def alloc_z(b):
+            s = st[b]
+            s["zg"] = grp.tile([P, N, PACK], BF16, name="zg", tag="zg", align_bytes=64)
+            s["z_codes"] = cod.tile([P, N], U32, name="z_codes", tag="z_codes", align_bytes=64)
+            s["z_scales"] = cod.tile([P, N], U8, name="z_scales", tag="z_scales", align_bytes=64)
 
         def m1(b, nb):
             s = st[b]
@@ -168,16 +191,16 @@ def tile_gcam_pb_t_kernel(tc, attention, v, x, wf, b_fuse, gamma, out):
                 op1=ALU.add,
             )
 
-        def qz(b, h):
+        def qz(b, lo, hi):
             s = st[b]
-            quantise(s["z_codes"], s["z_scales"], s["zg"], h * NH, (h + 1) * NH)
+            quantise(s["z_codes"], s["z_scales"], s["zg"], lo, hi, lo)
 
-        def m2(b, h):
+        def m2(b, lo, hi):
             s = st[b]
-            cols = slice(h * NH, (h + 1) * NH)
+            cols = slice(lo, hi)
             acc2 = ps_o.tile([P, NH], F32, name="acc2", tag="acc2")
             nc.tensor.matmul_mx(
-                out=acc2[:],
+                out=acc2[:, 0 : hi - lo],
                 lhsT=wf_codes[:, P : 2 * P].bitcast(FP8X4),
                 lhsT_scale=wf_scales[:, P : 2 * P],
                 rhs=s["x_codes"][:, cols].bitcast(FP8X4),
@@ -186,7 +209,7 @@ def tile_gcam_pb_t_kernel(tc, attention, v, x, wf, b_fuse, gamma, out):
                 stop=False,
             )
             nc.tensor.matmul_mx(
-                out=acc2[:],
+                out=acc2[:, 0 : hi - lo],
                 lhsT=wf_codes[:, 0:P].bitcast(FP8X4),
                 lhsT_scale=wf_scales[:, 0:P],
                 rhs=s["z_codes"][:, cols].bitcast(FP8X4),
@@ -194,93 +217,60 @@ def tile_gcam_pb_t_kernel(tc, attention, v, x, wf, b_fuse, gamma, out):
                 start=False,
                 stop=True,
             )
-            s["acc2", h] = acc2
+            s["acc2", lo] = acc2
 
-        def so(b, h):
+        def so(b, lo, hi):
             s = st[b]
-            cols = slice(h * NH, (h + 1) * NH)
+            if "out_sb" not in s:
+                s["out_sb"] = res.tile([P, N], F32, name="out_sb", tag="out_sb")
             nc.scalar.activation(
-                out=s["out_sb"][:, cols], in_=s["acc2", h][:], func=ACT.Identity,
+                out=s["out_sb"][:, lo:hi], in_=s["acc2", lo][:, 0 : hi - lo], func=ACT.Identity,
                 bias=bias_f[:, 0:1], scale=1.0,
             )
 
-        def period(i):
-            nxt = i + 1
-            more = nxt < B
-            s = st[i]
-            if more:
-                alloc_v(nxt)
-                regroup(nc.scalar.copy, st[nxt]["vg"], st[nxt]["v_raw"], 0, NH)
-                regroup(nc.scalar.copy, st[nxt]["vg"], st[nxt]["v_raw"], NH, N)
-                load_big(nxt + RAW_BUFS, "v_raw", v, 1)
-            s["zg"] = grp.tile([P, N, PACK], BF16, name="zg", tag="zg", align_bytes=64)
-            s["z_codes"] = cod.tile([P, N], U32, name="z_codes", tag="z_codes", align_bytes=64)
-            s["z_scales"] = cod.tile([P, N], U8, name="z_scales", tag="z_scales", align_bytes=64)
-            s["out_sb"] = res.tile([P, N], F32, name="out_sb", tag="out_sb")
-            tick_gx(i)
-            for nb in range(4):
-                m1(i, nb)
-            if more:
-                t_sa(nxt)
-                load_att(nxt + RAW_BUFS)
-            if i == 0:
-                stt(i, 0)
-                stt(i, 1)
-                stt(i, 2)
-                qv(i, 1)
-                for nb in range(3, 8):
-                    if nb + 1 < 8:
-                        m1(i, nb + 1)
-                    stt(i, nb)
-            else:
-                for nb in range(8):
-                    stt(i, nb)
-                    if nb + 4 < 8:
-                        m1(i, nb + 4)
-            if more:
-                alloc_x(nxt)
-                regroup(nc.scalar.copy, st[nxt]["xg"], st[nxt]["x_raw"], 0, XS)
-            qxs(i)
-            qz(i, 0)
-            m2(i, 0)
-            qz(i, 1)
-            qxg(i)
-            m2(i, 1)
-            for h in range(2):
-                so(i, h)
-                if not more:
-                    cols = slice(h * NH, (h + 1) * NH)
-                    nc.sync.dma_start(out=out[i][:, cols], in_=s["out_sb"][:, cols])
-            if more:
-                nc.sync.dma_start(out=out[i], in_=s["out_sb"][:])
-                qv(nxt, 0)
-                qa(nxt)
-                qv(nxt, 1)
-
-        gamma_b = consts.tile([P, 1], BF16, name="gamma_b")
-        nc.scalar.dma_start(out=gamma_b[:], in_=gamma.partition_broadcast(P))
-        bias_b = consts.tile([P, 1], BF16, name="bias_b")
-        with nc.allow_non_contiguous_dma(reason="one bias value a partition, 128 in all"):
-            nc.scalar.dma_start(out=bias_b[:], in_=b_fuse.rearrange("(o one) -> o one", one=1))
-        wf_raw = consts.tile([P, 2 * C], BF16, name="wf_raw")
-        load_att(0)
-        load_big(0, "v_raw", v, 2)
-        nc.scalar.dma_start(out=wf_raw[:], in_=wf)
-        load_big(0, "x_raw", x, 1)
-        for b in range(1, RAW_BUFS):
-            load_big(b, "v_raw", v, 1)
-            load_att(b)
-            load_big(b, "x_raw", x, 1)
+        def store(b, lo, hi):
+            nc.sync.dma_start(out=out[b][:, lo:hi], in_=st[b]["out_sb"][:, lo:hi])
 
         ident = consts.tile([P, P], F32, name="ident")
         make_identity(nc, ident[:])
+        gamma_b = consts.tile([P, 1], BF16, name="gamma_b")
+        nc.sync.dma_start(out=gamma_b[:], in_=gamma.partition_broadcast(P))
+        bias_b = consts.tile([P, 1], BF16, name="bias_b")
+        with nc.allow_non_contiguous_dma(reason="one bias value a partition, 128 in all"):
+            nc.sync.dma_start(out=bias_b[:], in_=b_fuse.rearrange("(o one) -> o one", one=1))
+        load_att(0, 2)
+        load_v(0, 4)
+        wf_raw = consts.tile([P, 2 * C], BF16, name="wf_raw")
+        nc.sync.dma_start(out=wf_raw[:], in_=wf)
+        load_x(0, XS, N)
+        load_att(1, 1)
+        load_v(1, 2)
+        load_x(0, 0, XS)
+        load_x(1, 0, N)
+        for b in range(2, RAW_BUFS):
+            load_v(b, 1)
+            load_att(b, 1)
+            load_x(b, 0, N)
+
+        t_sa(0)
+        load_att(RAW_BUFS, 1)
+        alloc_v(0)
+        alloc_ac(0)
+        rv(nc.vector.tensor_copy, 0, 0, NQ)
+        qv(0, 0, NQ)
+        qa(0, 0, NQ)
+        rv(nc.vector.tensor_copy, 0, NQ, NH)
+        qa(0, NQ, C)
+        qv(0, NQ, NH)
+        for nb in range(4):
+            m1(0, nb)
         gamma_f = consts.tile([P, 1], F32, name="gamma_f")
         nc.vector.tensor_copy(out=gamma_f[:], in_=gamma_b[:])
         bias_f = consts.tile([P, 1], F32, name="bias_f")
         nc.vector.tensor_copy(out=bias_f[:], in_=bias_b[:])
-
-        t_sa(0)
-        load_att(RAW_BUFS)
+        rv(nc.scalar.copy, 0, NH, NH + NQ)
+        rv(nc.scalar.copy, 0, NH + NQ, N)
+        load_v(RAW_BUFS, 1)
         wfg = consts.tile([P, 2 * O, PACK], BF16, name="wfg", align_bytes=64)
         wf_codes = consts.tile([P, 2 * O], U32, name="wf_codes", align_bytes=64)
         wf_scales = consts.tile([P, 2 * O], U8, name="wf_scales", align_bytes=64)
@@ -289,16 +279,98 @@ def tile_gcam_pb_t_kernel(tc, attention, v, x, wf, b_fuse, gamma, out):
             wfg[:].bitcast(F32),
             0,
         )
-        alloc_v(0)
-        regroup(nc.vector.tensor_copy, st[0]["vg"], st[0]["v_raw"], 0, 256)
-        regroup(nc.vector.tensor_copy, st[0]["vg"], st[0]["v_raw"], 256, NH)
-        regroup(nc.scalar.copy, st[0]["vg"], st[0]["v_raw"], NH, N)
-        load_big(RAW_BUFS, "v_raw", v, 1)
-        qv(0, 0)
-        qa(0)
-        quantise(wf_codes, wf_scales, wfg, 0, 2 * O)
-        alloc_x(0)
-        regroup(nc.scalar.copy, st[0]["xg"], st[0]["x_raw"], 0, XS)
 
-        for i in range(B):
-            period(i)
+        t_sa(1)
+        load_att(1 + RAW_BUFS, 1)
+        alloc_v(1)
+        rv(nc.scalar.copy, 1, 0, NH)
+        rv(nc.scalar.copy, 1, NH, N)
+        load_v(1 + RAW_BUFS, 1)
+        alloc_z(0)
+        alloc_xc(0)
+        tick_gx(0)
+        stt(0, 0)
+        stt(0, 1)
+        stt(0, 2)
+        qv(0, NH, N)
+        for nb in range(3, 8):
+            if nb + 1 < 8:
+                m1(0, nb + 1)
+            stt(0, nb)
+        quantise(wf_codes, wf_scales, wfg, 0, 2 * O, 0)
+        qv(1, 0, NH)
+        alloc_ac(1)
+        qa(1, 0, C)
+        for nb in range(4):
+            m1(1, nb)
+        qz(0, 0, NH)
+        qz(0, NH, N)
+        qxg(0)
+        m2(0, NH, N)
+        qv(1, NH, N)
+        sxs(0)
+        load_x(RAW_BUFS, 0, N)
+        alloc_xc(1)
+        sxs(1)
+        qxs(0)
+        m2(0, 0, NH)
+
+        for i in range(1, B - 1):
+            n = i + 1
+            so(i - 1, 0, NH)
+            so(i - 1, NH, N)
+            store(i - 1, 0, N)
+            alloc_v(n)
+            rv(nc.scalar.copy, n, 0, NH)
+            t_sa(n)
+            load_att(n + RAW_BUFS, 1)
+            rv(nc.scalar.copy, n, NH, N)
+            load_v(n + RAW_BUFS, 1)
+            alloc_z(i)
+            tick_gx(i)
+            for nb in range(8):
+                stt(i, nb)
+                if nb + 4 < 8:
+                    m1(i, nb + 4)
+            load_x(i + RAW_BUFS, 0, N)
+            alloc_xc(n)
+            sxs(n)
+            qv(n, 0, NH)
+            alloc_ac(n)
+            qa(n, 0, C)
+            for nb in range(4):
+                m1(n, nb)
+            qxs(i)
+            qz(i, 0, NH)
+            m2(i, 0, NH)
+            qz(i, NH, N)
+            qxg(i)
+            m2(i, NH, N)
+            qv(n, NH, N)
+
+        i = B - 1
+        so(i - 1, 0, NH)
+        so(i - 1, NH, N)
+        store(i - 1, 0, N)
+        alloc_z(i)
+        tick_gx(i)
+        for nb in range(6):
+            stt(i, nb)
+            if nb + 4 < 8:
+                m1(i, nb + 4)
+        qxs(i)
+        qz(i, 0, NH)
+        m2(i, 0, NH)
+        so(i, 0, NH)
+        store(i, 0, NH)
+        qxg(i)
+        qz(i, NH, NH + NQ)
+        m2(i, NH, NH + NQ)
+        so(i, NH, NH + NQ)
+        store(i, NH, NH + NQ)
+        stt(i, 6)
+        stt(i, 7)
+        qz(i, NH + NQ, N)
+        m2(i, NH + NQ, N)
+        so(i, NH + NQ, N)
+        store(i, NH + NQ, N)

@@ -108,10 +108,25 @@ def tile_gcam_pb_t_kernel(tc, attention, v, x, wf, b_fuse, gamma, out):
             s["x_codes"] = cod.tile([P, N], U32, name="x_codes", tag="x_codes", align_bytes=64)
             s["x_scales"] = cod.tile([P, N], U8, name="x_scales", tag="x_scales", align_bytes=64)
 
+        def px(b):
+            s = st[b]
+            for h in range(XS // NQ):
+                tp = ps_t.tile([P, NQ, PACK], BF16, name="tp", tag="tp")
+                for lo in range(0, NQ, NB):
+                    nc.tensor.matmul(
+                        tp[:, lo : lo + NB, :].rearrange("p n t -> p (n t)"),
+                        lhsT=ident_b[:],
+                        rhs=s["x_raw"][:, :, h * NQ + lo : h * NQ + lo + NB].rearrange("p t n -> p n t"),
+                        start=True,
+                        stop=True,
+                    )
+                s["xp", h] = tp
+
         def sxs(b):
             s = st[b]
             s["xg"] = grp.tile([P, XS, PACK], BF16, name="xg", tag="xg", align_bytes=64)
-            regroup(nc.scalar.copy, s["xg"], s["x_raw"], 0, XS, 0)
+            for h in range(XS // NQ):
+                nc.scalar.copy(out=s["xg"][:, h * NQ : (h + 1) * NQ, :], in_=s["xp", h][:])
 
         def t_sa(b):
             s = st[b]
@@ -233,6 +248,8 @@ def tile_gcam_pb_t_kernel(tc, attention, v, x, wf, b_fuse, gamma, out):
 
         ident = consts.tile([P, P], F32, name="ident")
         make_identity(nc, ident[:])
+        ident_b = consts.tile([P, P], BF16, name="ident_b")
+        make_identity(nc, ident_b[:])
         gamma_b = consts.tile([P, 1], BF16, name="gamma_b")
         nc.sync.dma_start(out=gamma_b[:], in_=gamma.partition_broadcast(P))
         bias_b = consts.tile([P, 1], BF16, name="bias_b")
@@ -257,20 +274,16 @@ def tile_gcam_pb_t_kernel(tc, attention, v, x, wf, b_fuse, gamma, out):
         alloc_v(0)
         alloc_ac(0)
         rv(nc.vector.tensor_copy, 0, 0, NQ)
+        rv(nc.vector.tensor_copy, 0, NQ, NH)
         qv(0, 0, NQ)
         qa(0, 0, NQ)
-        rv(nc.vector.tensor_copy, 0, NQ, NH)
         qa(0, NQ, C)
         qv(0, NQ, NH)
-        for nb in range(4):
-            m1(0, nb)
-        gamma_f = consts.tile([P, 1], F32, name="gamma_f")
-        nc.vector.tensor_copy(out=gamma_f[:], in_=gamma_b[:])
-        bias_f = consts.tile([P, 1], F32, name="bias_f")
-        nc.vector.tensor_copy(out=bias_f[:], in_=bias_b[:])
         rv(nc.scalar.copy, 0, NH, NH + NQ)
         rv(nc.scalar.copy, 0, NH + NQ, N)
         load_v(RAW_BUFS, 1)
+        m1(0, 0)
+        m1(0, 1)
         wfg = consts.tile([P, 2 * O, PACK], BF16, name="wfg", align_bytes=64)
         wf_codes = consts.tile([P, 2 * O], U32, name="wf_codes", align_bytes=64)
         wf_scales = consts.tile([P, 2 * O], U8, name="wf_scales", align_bytes=64)
@@ -279,6 +292,12 @@ def tile_gcam_pb_t_kernel(tc, attention, v, x, wf, b_fuse, gamma, out):
             wfg[:].bitcast(F32),
             0,
         )
+        m1(0, 2)
+        m1(0, 3)
+        gamma_f = consts.tile([P, 1], F32, name="gamma_f")
+        nc.vector.tensor_copy(out=gamma_f[:], in_=gamma_b[:])
+        bias_f = consts.tile([P, 1], F32, name="bias_f")
+        nc.vector.tensor_copy(out=bias_f[:], in_=bias_b[:])
 
         t_sa(1)
         load_att(1 + RAW_BUFS, 1)
@@ -288,15 +307,19 @@ def tile_gcam_pb_t_kernel(tc, attention, v, x, wf, b_fuse, gamma, out):
         load_v(1 + RAW_BUFS, 1)
         alloc_z(0)
         alloc_xc(0)
+        qv(0, NH, NH + NQ)
         tick_gx(0)
         stt(0, 0)
         stt(0, 1)
         stt(0, 2)
-        qv(0, NH, N)
+        qv(0, NH + NQ, N)
         for nb in range(3, 8):
             if nb + 1 < 8:
                 m1(0, nb + 1)
             stt(0, nb)
+        px(0)
+        sxs(0)
+        load_x(RAW_BUFS, 0, N)
         quantise(wf_codes, wf_scales, wfg, 0, 2 * O, 0)
         qv(1, 0, NH)
         alloc_ac(1)
@@ -305,13 +328,12 @@ def tile_gcam_pb_t_kernel(tc, attention, v, x, wf, b_fuse, gamma, out):
             m1(1, nb)
         qz(0, 0, NH)
         qz(0, NH, N)
+        alloc_xc(1)
+        px(1)
+        sxs(1)
         qxg(0)
         m2(0, NH, N)
         qv(1, NH, N)
-        sxs(0)
-        load_x(RAW_BUFS, 0, N)
-        alloc_xc(1)
-        sxs(1)
         qxs(0)
         m2(0, 0, NH)
 
@@ -322,16 +344,17 @@ def tile_gcam_pb_t_kernel(tc, attention, v, x, wf, b_fuse, gamma, out):
             store(i - 1, 0, N)
             alloc_v(n)
             rv(nc.scalar.copy, n, 0, NH)
-            t_sa(n)
-            load_att(n + RAW_BUFS, 1)
-            rv(nc.scalar.copy, n, NH, N)
-            load_v(n + RAW_BUFS, 1)
             alloc_z(i)
             tick_gx(i)
             for nb in range(8):
                 stt(i, nb)
                 if nb + 4 < 8:
                     m1(i, nb + 4)
+            t_sa(n)
+            load_att(n + RAW_BUFS, 1)
+            rv(nc.scalar.copy, n, NH, N)
+            load_v(n + RAW_BUFS, 1)
+            px(n)
             load_x(i + RAW_BUFS, 0, N)
             alloc_xc(n)
             sxs(n)

@@ -114,9 +114,9 @@ def tile_gcam_pb_t_kernel(tc, attention, v, x, wf, b_fuse, gamma, out):
                 tp = ps_t.tile([P, NQ, PACK], BF16, name="tp", tag="tp")
                 for lo in range(0, NQ, NB):
                     nc.tensor.matmul(
-                        tp[:, lo : lo + NB, :].rearrange("p n t -> p (n t)"),
+                        tp[:, lo : lo + NB, :].rearrange("p n t -> p t n"),
                         lhsT=ident_b[:],
-                        rhs=s["x_raw"][:, :, h * NQ + lo : h * NQ + lo + NB].rearrange("p t n -> p n t"),
+                        rhs=s["x_raw"][:, :, h * NQ + lo : h * NQ + lo + NB],
                         start=True,
                         stop=True,
                     )
@@ -126,7 +126,10 @@ def tile_gcam_pb_t_kernel(tc, attention, v, x, wf, b_fuse, gamma, out):
             s = st[b]
             s["xg"] = grp.tile([P, XS, PACK], BF16, name="xg", tag="xg", align_bytes=64)
             for h in range(XS // NQ):
-                nc.scalar.copy(out=s["xg"][:, h * NQ : (h + 1) * NQ, :], in_=s["xp", h][:])
+                nc.scalar.copy(
+                    out=s["xg"][:, h * NQ : (h + 1) * NQ, :].rearrange("p n t -> p (n t)").bitcast(F32),
+                    in_=s["xp", h][:].rearrange("p n t -> p (n t)").bitcast(F32),
+                )
 
         def t_sa(b):
             s = st[b]

@@ -17,9 +17,9 @@ PACK = 4
 NB = 128
 NH = 512
 NQ = 256
-XG = 512
+XG = 416
 XS = N - XG
-GW = 128
+GW = 104
 RAW_BUFS = 4
 FLOPS = 2 * B * C * C * N + 2 * B * O * 2 * C * N
 
@@ -32,9 +32,9 @@ def tile_gcam_pb_t_kernel(tc, attention, v, x, wf, b_fuse, gamma, out):
         grp = ctx.enter_context(tc.tile_pool(name="grp", bufs=2))
         cod = ctx.enter_context(tc.tile_pool(name="cod", bufs=2))
         res = ctx.enter_context(tc.tile_pool(name="res", bufs=4))
-        ps_t = ctx.enter_context(tc.psum_pool(name="ps_t", bufs=2))
+        ps_t = ctx.enter_context(tc.psum_pool(name="ps_t", bufs=3))
         ps_a = ctx.enter_context(tc.psum_pool(name="ps_a", bufs=4))
-        ps_o = ctx.enter_context(tc.psum_pool(name="ps_o", bufs=2))
+        ps_o = ctx.enter_context(tc.psum_pool(name="ps_o", bufs=1))
         ctx.enter_context(tc.manual_schedule())
 
         st = {}
@@ -76,15 +76,14 @@ def tile_gcam_pb_t_kernel(tc, attention, v, x, wf, b_fuse, gamma, out):
                 nc.sync.dma_start(out=t[:, k * w : (k + 1) * w, :], in_=view[:, k * w : (k + 1) * w, :])
             st[b]["att_raw"] = t
 
-        def load_v(b, pieces):
+        def load_v(b, edges):
             if b >= B:
                 return
-            t = raw.tile([P, PACK, N], BF16, name="v_raw", tag="v_raw")
+            if "v_raw" not in st[b]:
+                st[b]["v_raw"] = raw.tile([P, PACK, N], BF16, name="v_raw", tag="v_raw")
             view = v[b].rearrange("(p t) n -> p t n", t=PACK)
-            w = N // pieces
-            for k in range(pieces):
-                nc.sync.dma_start(out=t[:, :, k * w : (k + 1) * w], in_=view[:, :, k * w : (k + 1) * w])
-            st[b]["v_raw"] = t
+            for lo, hi in zip(edges, edges[1:]):
+                nc.sync.dma_start(out=st[b]["v_raw"][:, :, lo:hi], in_=view[:, :, lo:hi])
 
         def load_x(b, lo, hi):
             if b >= B:
@@ -107,29 +106,35 @@ def tile_gcam_pb_t_kernel(tc, attention, v, x, wf, b_fuse, gamma, out):
             s = st[b]
             s["x_codes"] = cod.tile([P, N], U32, name="x_codes", tag="x_codes", align_bytes=64)
             s["x_scales"] = cod.tile([P, N], U8, name="x_scales", tag="x_scales", align_bytes=64)
+            s["xg"] = grp.tile([P, N, PACK], BF16, name="xg", tag="xg", align_bytes=64)
 
-        def px(b):
+        def px(b, h):
             s = st[b]
-            for h in range(XS // NQ):
-                tp = ps_t.tile([P, NQ, PACK], BF16, name="tp", tag="tp")
-                for lo in range(0, NQ, NB):
-                    nc.tensor.matmul(
-                        tp[:, lo : lo + NB, :].rearrange("p n t -> p t n"),
-                        lhsT=ident_b[:],
-                        rhs=s["x_raw"][:, :, h * NQ + lo : h * NQ + lo + NB],
-                        start=True,
-                        stop=True,
-                    )
-                s["xp", h] = tp
-
-        def sxs(b):
-            s = st[b]
-            s["xg"] = grp.tile([P, XS, PACK], BF16, name="xg", tag="xg", align_bytes=64)
-            for h in range(XS // NQ):
-                nc.scalar.copy(
-                    out=s["xg"][:, h * NQ : (h + 1) * NQ, :].rearrange("p n t -> p (n t)").bitcast(F32),
-                    in_=s["xp", h][:].rearrange("p n t -> p (n t)").bitcast(F32),
+            top = min(h + NQ, XS)
+            tp = ps_t.tile([P, NQ, PACK], BF16, name="tp", tag="tp")
+            for lo in range(h, top, NB):
+                hi = min(lo + NB, top)
+                nc.tensor.matmul(
+                    tp[:, lo - h : hi - h, :].rearrange("p n t -> p t n"),
+                    lhsT=ident_b[:],
+                    rhs=s["x_raw"][:, :, lo:hi],
+                    start=True,
+                    stop=True,
                 )
+            s["xp", h] = tp
+
+        def sx(b, h):
+            s = st[b]
+            top = min(h + NQ, XS)
+            nc.scalar.copy(
+                out=s["xg"][:, h:top, :].rearrange("p n t -> p (n t)").bitcast(F32),
+                in_=s["xp", h][:, 0 : top - h, :].rearrange("p n t -> p (n t)").bitcast(F32),
+            )
+
+        def pxs(b):
+            for h in range(0, XS, NQ):
+                px(b, h)
+                sx(b, h)
 
         def t_sa(b):
             s = st[b]
@@ -151,28 +156,25 @@ def tile_gcam_pb_t_kernel(tc, attention, v, x, wf, b_fuse, gamma, out):
             s = st[b]
             quantise(s["v_codes"], s["v_scales"], s["vg"], lo, hi, lo)
 
-        def qxs(b):
+        def qx(b, lo, hi):
             s = st[b]
-            quantise(s["x_codes"], s["x_scales"], s["xg"], 0, XS, 0)
+            quantise(s["x_codes"], s["x_scales"], s["xg"], lo, hi, lo)
 
-        def qxg(b):
-            s = st[b]
-            quantise(s["x_codes"], s["x_scales"], s["xgg"], XS, N, 0)
-
-        def tick_gx(b):
+        def tick_gx(b, then=None):
             s = st[b]
             tick = grp.tile([P, 1], F32, name="tick", tag="tick")
             nc.vector.memset(tick[:], 1.0)
-            s["xgg"] = grp.tile([P, XG, PACK], BF16, name="xgg", tag="xgg", align_bytes=64)
-            for lo in range(0, XG, GW):
+            for lo in range(XS, N, GW):
                 nc.gpsimd.tensor_scalar(
-                    out=s["xgg"][:, lo : lo + GW, :],
-                    in0=s["x_raw"][:, :, XS + lo : XS + lo + GW].rearrange("p t n -> p n t"),
+                    out=s["xg"][:, lo : lo + GW, :],
+                    in0=s["x_raw"][:, :, lo : lo + GW].rearrange("p t n -> p n t"),
                     scalar1=tick[:, 0:1],
                     scalar2=0.0,
                     op0=ALU.mult,
                     op1=ALU.add,
                 )
+                if lo == XS and then is not None:
+                    then()
 
         def alloc_z(b):
             s = st[b]
@@ -207,6 +209,21 @@ def tile_gcam_pb_t_kernel(tc, attention, v, x, wf, b_fuse, gamma, out):
                 in1=s["vg"][:, cols, :],
                 op0=ALU.mult,
                 op1=ALU.add,
+            )
+
+        def zs(b, nb):
+            s = st[b]
+            s["zt"] = grp.tile([P, NB, PACK], F32, name="zt", tag="zt")
+            nc.scalar.activation(
+                out=s["zt"][:], in_=s["acc", nb][:].rearrange("p t n -> p n t"), func=ACT.Copy,
+                scale=gamma_f[:, 0:1],
+            )
+
+        def za(b, nb):
+            s = st[b]
+            cols = slice(nb * NB, (nb + 1) * NB)
+            nc.gpsimd.tensor_tensor(
+                out=s["zg"][:, cols, :], in0=s["zt"][:], in1=s["vg"][:, cols, :], op=ALU.add
             )
 
         def qz(b, lo, hi):
@@ -253,22 +270,22 @@ def tile_gcam_pb_t_kernel(tc, attention, v, x, wf, b_fuse, gamma, out):
         make_identity(nc, ident[:])
         ident_b = consts.tile([P, P], BF16, name="ident_b")
         make_identity(nc, ident_b[:])
+        load_att(0, 2)
+        load_v(0, (0, NQ, NH, NH + NQ, N))
         gamma_b = consts.tile([P, 1], BF16, name="gamma_b")
         nc.sync.dma_start(out=gamma_b[:], in_=gamma.partition_broadcast(P))
-        bias_b = consts.tile([P, 1], BF16, name="bias_b")
-        with nc.allow_non_contiguous_dma(reason="one bias value a partition, 128 in all"):
-            nc.sync.dma_start(out=bias_b[:], in_=b_fuse.rearrange("(o one) -> o one", one=1))
-        load_att(0, 2)
-        load_v(0, 4)
         wf_raw = consts.tile([P, 2 * C], BF16, name="wf_raw")
         nc.sync.dma_start(out=wf_raw[:], in_=wf)
         load_x(0, XS, N)
         load_att(1, 1)
-        load_v(1, 2)
+        load_v(1, (0, NH, N))
         load_x(0, 0, XS)
         load_x(1, 0, N)
+        bias_b = consts.tile([P, 1], BF16, name="bias_b")
+        with nc.allow_non_contiguous_dma(reason="one bias value a partition, 128 in all"):
+            nc.sync.dma_start(out=bias_b[:], in_=b_fuse.rearrange("(o one) -> o one", one=1))
         for b in range(2, RAW_BUFS):
-            load_v(b, 1)
+            load_v(b, (0, N))
             load_att(b, 1)
             load_x(b, 0, N)
 
@@ -284,7 +301,7 @@ def tile_gcam_pb_t_kernel(tc, attention, v, x, wf, b_fuse, gamma, out):
         qv(0, NQ, NH)
         rv(nc.scalar.copy, 0, NH, NH + NQ)
         rv(nc.scalar.copy, 0, NH + NQ, N)
-        load_v(RAW_BUFS, 1)
+        load_v(RAW_BUFS, (0, N))
         m1(0, 0)
         m1(0, 1)
         wfg = consts.tile([P, 2 * O, PACK], BF16, name="wfg", align_bytes=64)
@@ -300,14 +317,11 @@ def tile_gcam_pb_t_kernel(tc, attention, v, x, wf, b_fuse, gamma, out):
         gamma_f = consts.tile([P, 1], F32, name="gamma_f")
         nc.vector.tensor_copy(out=gamma_f[:], in_=gamma_b[:])
         bias_f = consts.tile([P, 1], F32, name="bias_f")
-        nc.vector.tensor_copy(out=bias_f[:], in_=bias_b[:])
 
         t_sa(1)
         load_att(1 + RAW_BUFS, 1)
         alloc_v(1)
         rv(nc.scalar.copy, 1, 0, NH)
-        rv(nc.scalar.copy, 1, NH, N)
-        load_v(1 + RAW_BUFS, 1)
         alloc_z(0)
         alloc_xc(0)
         qv(0, NH, NH + NQ)
@@ -320,8 +334,9 @@ def tile_gcam_pb_t_kernel(tc, attention, v, x, wf, b_fuse, gamma, out):
             if nb + 1 < 8:
                 m1(0, nb + 1)
             stt(0, nb)
-        px(0)
-        sxs(0)
+        pxs(0)
+        rv(nc.scalar.copy, 1, NH, N)
+        load_v(1 + RAW_BUFS, (0, N))
         load_x(RAW_BUFS, 0, N)
         quantise(wf_codes, wf_scales, wfg, 0, 2 * O, 0)
         qv(1, 0, NH)
@@ -329,67 +344,75 @@ def tile_gcam_pb_t_kernel(tc, attention, v, x, wf, b_fuse, gamma, out):
         qa(1, 0, C)
         for nb in range(4):
             m1(1, nb)
+        zs(1, 0)
         qz(0, 0, NH)
         qz(0, NH, N)
+        nc.vector.tensor_copy(out=bias_f[:], in_=bias_b[:])
         alloc_xc(1)
-        px(1)
-        sxs(1)
-        qxg(0)
-        m2(0, NH, N)
-        qv(1, NH, N)
-        qxs(0)
+        pxs(1)
+        qx(0, 0, NH)
         m2(0, 0, NH)
+        qv(1, NH, N)
+        so(0, 0, NH)
+        qx(0, NH, N)
+        m2(0, NH, N)
 
         for i in range(1, B - 1):
             n = i + 1
-            so(i - 1, 0, NH)
-            so(i - 1, NH, N)
-            store(i - 1, 0, N)
+            m1(i, 4)
             alloc_v(n)
             rv(nc.scalar.copy, n, 0, NH)
+            so(i - 1, NH, N)
+            store(i - 1, 0, N)
             alloc_z(i)
-            tick_gx(i)
-            for nb in range(8):
+            alloc_xc(n)
+            tick_gx(i, lambda: za(i, 0))
+            for nb in range(1, 8):
                 stt(i, nb)
                 if nb + 4 < 8:
                     m1(i, nb + 4)
+            px(n, 0)
+            sx(n, 0)
             t_sa(n)
             load_att(n + RAW_BUFS, 1)
+            px(n, NQ)
+            px(n, 2 * NQ)
             rv(nc.scalar.copy, n, NH, N)
-            load_v(n + RAW_BUFS, 1)
-            px(n)
+            load_v(n + RAW_BUFS, (0, N))
+            sx(n, NQ)
+            sx(n, 2 * NQ)
             load_x(i + RAW_BUFS, 0, N)
-            alloc_xc(n)
-            sxs(n)
             qv(n, 0, NH)
+            qx(i, 0, NH)
+            qz(i, 0, NH)
+            m2(i, 0, NH)
+            so(i, 0, NH)
             alloc_ac(n)
             qa(n, 0, C)
             for nb in range(4):
                 m1(n, nb)
-            qxs(i)
-            qz(i, 0, NH)
-            m2(i, 0, NH)
+            zs(n, 0)
             qz(i, NH, N)
-            qxg(i)
+            qx(i, NH, N)
             m2(i, NH, N)
             qv(n, NH, N)
 
         i = B - 1
-        so(i - 1, 0, NH)
         so(i - 1, NH, N)
         store(i - 1, 0, N)
         alloc_z(i)
-        tick_gx(i)
-        for nb in range(6):
+        tick_gx(i, lambda: za(i, 0))
+        m1(i, 4)
+        for nb in range(1, 6):
             stt(i, nb)
             if nb + 4 < 8:
                 m1(i, nb + 4)
-        qxs(i)
+        qx(i, 0, NH)
         qz(i, 0, NH)
         m2(i, 0, NH)
         so(i, 0, NH)
         store(i, 0, NH)
-        qxg(i)
+        qx(i, NH, N)
         qz(i, NH, NH + NQ)
         m2(i, NH, NH + NQ)
         so(i, NH, NH + NQ)

@@ -17,9 +17,9 @@ PACK = 4
 NB = 128
 NH = 512
 NQ = 256
-XG = 416
+XG = 512
 XS = N - XG
-GW = 104
+GW = 128
 RAW_BUFS = 4
 FLOPS = 2 * B * C * C * N + 2 * B * O * 2 * C * N
 
@@ -32,9 +32,9 @@ def tile_gcam_pb_t_kernel(tc, attention, v, x, wf, b_fuse, gamma, out):
         grp = ctx.enter_context(tc.tile_pool(name="grp", bufs=2))
         cod = ctx.enter_context(tc.tile_pool(name="cod", bufs=2))
         res = ctx.enter_context(tc.tile_pool(name="res", bufs=4))
-        ps_t = ctx.enter_context(tc.psum_pool(name="ps_t", bufs=3))
+        ps_t = ctx.enter_context(tc.psum_pool(name="ps_t", bufs=2))
         ps_a = ctx.enter_context(tc.psum_pool(name="ps_a", bufs=4))
-        ps_o = ctx.enter_context(tc.psum_pool(name="ps_o", bufs=1))
+        ps_o = ctx.enter_context(tc.psum_pool(name="ps_o", bufs=2))
         ctx.enter_context(tc.manual_schedule())
 
         st = {}
@@ -213,9 +213,10 @@ def tile_gcam_pb_t_kernel(tc, attention, v, x, wf, b_fuse, gamma, out):
 
         def zs(b, nb):
             s = st[b]
-            s["zt"] = grp.tile([P, NB, PACK], F32, name="zt", tag="zt")
+            zt = grp.tile([P, NB, PACK], F32, name="zt", tag="zt")
+            s["zt", nb] = zt
             nc.scalar.activation(
-                out=s["zt"][:], in_=s["acc", nb][:].rearrange("p t n -> p n t"), func=ACT.Copy,
+                out=zt[:], in_=s["acc", nb][:].rearrange("p t n -> p n t"), func=ACT.Copy,
                 scale=gamma_f[:, 0:1],
             )
 
@@ -223,17 +224,17 @@ def tile_gcam_pb_t_kernel(tc, attention, v, x, wf, b_fuse, gamma, out):
             s = st[b]
             cols = slice(nb * NB, (nb + 1) * NB)
             nc.gpsimd.tensor_tensor(
-                out=s["zg"][:, cols, :], in0=s["zt"][:], in1=s["vg"][:, cols, :], op=ALU.add
+                out=s["zg"][:, cols, :], in0=s["zt", nb][:], in1=s["vg"][:, cols, :], op=ALU.add
             )
 
         def qz(b, lo, hi):
             s = st[b]
             quantise(s["z_codes"], s["z_scales"], s["zg"], lo, hi, lo)
 
-        def m2(b, lo, hi):
+        def m2x(b, lo, hi, pool, tag):
             s = st[b]
             cols = slice(lo, hi)
-            acc2 = ps_o.tile([P, NH], F32, name="acc2", tag="acc2")
+            acc2 = pool.tile([P, NH], F32, name="acc2", tag=tag)
             nc.tensor.matmul_mx(
                 out=acc2[:, 0 : hi - lo],
                 lhsT=wf_codes[:, P : 2 * P].bitcast(FP8X4),
@@ -243,8 +244,13 @@ def tile_gcam_pb_t_kernel(tc, attention, v, x, wf, b_fuse, gamma, out):
                 start=True,
                 stop=False,
             )
+            s["acc2", lo] = acc2
+
+        def m2z(b, lo, hi):
+            s = st[b]
+            cols = slice(lo, hi)
             nc.tensor.matmul_mx(
-                out=acc2[:, 0 : hi - lo],
+                out=s["acc2", lo][:, 0 : hi - lo],
                 lhsT=wf_codes[:, 0:P].bitcast(FP8X4),
                 lhsT_scale=wf_scales[:, 0:P],
                 rhs=s["z_codes"][:, cols].bitcast(FP8X4),
@@ -252,7 +258,10 @@ def tile_gcam_pb_t_kernel(tc, attention, v, x, wf, b_fuse, gamma, out):
                 start=False,
                 stop=True,
             )
-            s["acc2", lo] = acc2
+
+        def m2(b, lo, hi):
+            m2x(b, lo, hi, ps_o, "acc2")
+            m2z(b, lo, hi)
 
         def so(b, lo, hi):
             s = st[b]
@@ -344,7 +353,6 @@ def tile_gcam_pb_t_kernel(tc, attention, v, x, wf, b_fuse, gamma, out):
         qa(1, 0, C)
         for nb in range(4):
             m1(1, nb)
-        zs(1, 0)
         qz(0, 0, NH)
         qz(0, NH, N)
         nc.vector.tensor_copy(out=bias_f[:], in_=bias_b[:])
@@ -359,28 +367,25 @@ def tile_gcam_pb_t_kernel(tc, attention, v, x, wf, b_fuse, gamma, out):
 
         for i in range(1, B - 1):
             n = i + 1
-            m1(i, 4)
             alloc_v(n)
             rv(nc.scalar.copy, n, 0, NH)
             so(i - 1, NH, N)
             store(i - 1, 0, N)
             alloc_z(i)
             alloc_xc(n)
-            tick_gx(i, lambda: za(i, 0))
-            for nb in range(1, 8):
+            tick_gx(i)
+            for nb in range(8):
                 stt(i, nb)
                 if nb + 4 < 8:
                     m1(i, nb + 4)
-            px(n, 0)
-            sx(n, 0)
             t_sa(n)
             load_att(n + RAW_BUFS, 1)
+            px(n, 0)
             px(n, NQ)
-            px(n, 2 * NQ)
             rv(nc.scalar.copy, n, NH, N)
             load_v(n + RAW_BUFS, (0, N))
+            sx(n, 0)
             sx(n, NQ)
-            sx(n, 2 * NQ)
             load_x(i + RAW_BUFS, 0, N)
             qv(n, 0, NH)
             qx(i, 0, NH)
@@ -391,35 +396,40 @@ def tile_gcam_pb_t_kernel(tc, attention, v, x, wf, b_fuse, gamma, out):
             qa(n, 0, C)
             for nb in range(4):
                 m1(n, nb)
-            zs(n, 0)
             qz(i, NH, N)
             qx(i, NH, N)
             m2(i, NH, N)
             qv(n, NH, N)
 
         i = B - 1
+        zs(i, 0)
+        m1(i, 4)
+        zs(i, 1)
+        m1(i, 5)
         so(i - 1, NH, N)
         store(i - 1, 0, N)
+        regroup(nc.scalar.copy, st[i]["xg"], st[i]["x_raw"], XS, N, XS)
         alloc_z(i)
-        tick_gx(i, lambda: za(i, 0))
-        m1(i, 4)
-        for nb in range(1, 6):
+        za(i, 0)
+        za(i, 1)
+        for nb in range(2, 8):
             stt(i, nb)
             if nb + 4 < 8:
                 m1(i, nb + 4)
-        qx(i, 0, NH)
-        qz(i, 0, NH)
-        m2(i, 0, NH)
-        so(i, 0, NH)
-        store(i, 0, NH)
         qx(i, NH, N)
-        qz(i, NH, NH + NQ)
-        m2(i, NH, NH + NQ)
-        so(i, NH, NH + NQ)
-        store(i, NH, NH + NQ)
-        stt(i, 6)
-        stt(i, 7)
-        qz(i, NH + NQ, N)
-        m2(i, NH + NQ, N)
-        so(i, NH + NQ, N)
-        store(i, NH + NQ, N)
+        m2x(i, NH, N, ps_a, "acc")
+        qz(i, NH, N)
+        m2z(i, NH, N)
+        so(i, NH, N)
+        store(i, NH, N)
+        qx(i, 0, NH)
+        m2x(i, 0, NQ, ps_a, "acc")
+        m2x(i, NQ, NH, ps_a, "acc")
+        qz(i, 0, NQ)
+        m2z(i, 0, NQ)
+        so(i, 0, NQ)
+        store(i, 0, NQ)
+        qz(i, NQ, NH)
+        m2z(i, NQ, NH)
+        so(i, NQ, NH)
+        store(i, NQ, NH)

@@ -108,9 +108,12 @@ def tile_gcam_pb_t_kernel(tc, attention, v, x, wf, b_fuse, gamma, out):
             s["x_scales"] = cod.tile([P, N], U8, name="x_scales", tag="x_scales", align_bytes=64)
             s["xg"] = grp.tile([P, N, PACK], BF16, name="xg", tag="xg", align_bytes=64)
 
+        def split(b):
+            return 712 if b in (2, 4, 6) else XS
+
         def px(b, h):
             s = st[b]
-            top = min(h + NQ, XS)
+            top = min(h + NQ, split(b))
             tp = ps_t.tile([P, NQ, PACK], BF16, name="tp", tag="tp")
             for lo in range(h, top, NB):
                 hi = min(lo + NB, top)
@@ -125,7 +128,7 @@ def tile_gcam_pb_t_kernel(tc, attention, v, x, wf, b_fuse, gamma, out):
 
         def sx(b, h):
             s = st[b]
-            top = min(h + NQ, XS)
+            top = min(h + NQ, split(b))
             nc.scalar.copy(
                 out=s["xg"][:, h:top, :].rearrange("p n t -> p (n t)").bitcast(F32),
                 in_=s["xp", h][:, 0 : top - h, :].rearrange("p n t -> p (n t)").bitcast(F32),
@@ -164,16 +167,17 @@ def tile_gcam_pb_t_kernel(tc, attention, v, x, wf, b_fuse, gamma, out):
             s = st[b]
             tick = grp.tile([P, 1], F32, name="tick", tag="tick")
             nc.vector.memset(tick[:], 1.0)
-            for lo in range(XS, N, GW):
+            gw = GW if split(b) == XS else 104
+            for lo in range(split(b), N, gw):
                 nc.gpsimd.tensor_scalar(
-                    out=s["xg"][:, lo : lo + GW, :],
-                    in0=s["x_raw"][:, :, lo : lo + GW].rearrange("p t n -> p n t"),
+                    out=s["xg"][:, lo : lo + gw, :],
+                    in0=s["x_raw"][:, :, lo : lo + gw].rearrange("p t n -> p n t"),
                     scalar1=tick[:, 0:1],
                     scalar2=0.0,
                     op0=ALU.mult,
                     op1=ALU.add,
                 )
-                if lo == XS and then is not None:
+                if lo == split(b) and then is not None:
                     then()
 
         def alloc_z(b):
@@ -285,9 +289,9 @@ def tile_gcam_pb_t_kernel(tc, attention, v, x, wf, b_fuse, gamma, out):
         nc.sync.dma_start(out=gamma_b[:], in_=gamma.partition_broadcast(P))
         wf_raw = consts.tile([P, 2 * C], BF16, name="wf_raw")
         nc.sync.dma_start(out=wf_raw[:], in_=wf)
+        load_v(1, (0, NH, N))
         load_x(0, XS, N)
         load_att(1, 1)
-        load_v(1, (0, NH, N))
         load_x(0, 0, XS)
         load_x(1, 0, N)
         bias_b = consts.tile([P, 1], BF16, name="bias_b")
@@ -313,6 +317,22 @@ def tile_gcam_pb_t_kernel(tc, attention, v, x, wf, b_fuse, gamma, out):
         load_v(RAW_BUFS, (0, N))
         m1(0, 0)
         m1(0, 1)
+        m1(0, 2)
+        m1(0, 3)
+        gamma_f = consts.tile([P, 1], F32, name="gamma_f")
+        nc.vector.tensor_copy(out=gamma_f[:], in_=gamma_b[:])
+        bias_f = consts.tile([P, 1], F32, name="bias_f")
+
+        alloc_z(0)
+        alloc_xc(0)
+        qv(0, NH, NH + NQ)
+        tick_gx(0)
+        stt(0, 0)
+        m1(0, 4)
+        stt(0, 1)
+        m1(0, 5)
+        alloc_v(1)
+        rv(nc.scalar.copy, 1, 0, NH)
         wfg = consts.tile([P, 2 * O, PACK], BF16, name="wfg", align_bytes=64)
         wf_codes = consts.tile([P, 2 * O], U32, name="wf_codes", align_bytes=64)
         wf_scales = consts.tile([P, 2 * O], U8, name="wf_scales", align_bytes=64)
@@ -321,27 +341,14 @@ def tile_gcam_pb_t_kernel(tc, attention, v, x, wf, b_fuse, gamma, out):
             wfg[:].bitcast(F32),
             0,
         )
-        m1(0, 2)
-        m1(0, 3)
-        gamma_f = consts.tile([P, 1], F32, name="gamma_f")
-        nc.vector.tensor_copy(out=gamma_f[:], in_=gamma_b[:])
-        bias_f = consts.tile([P, 1], F32, name="bias_f")
-
-        t_sa(1)
-        load_att(1 + RAW_BUFS, 1)
-        alloc_v(1)
-        rv(nc.scalar.copy, 1, 0, NH)
-        alloc_z(0)
-        alloc_xc(0)
-        qv(0, NH, NH + NQ)
-        tick_gx(0)
-        stt(0, 0)
-        stt(0, 1)
         stt(0, 2)
         qv(0, NH + NQ, N)
-        for nb in range(3, 8):
-            if nb + 1 < 8:
-                m1(0, nb + 1)
+        m1(0, 6)
+        stt(0, 3)
+        m1(0, 7)
+        t_sa(1)
+        load_att(1 + RAW_BUFS, 1)
+        for nb in range(4, 8):
             stt(0, nb)
         pxs(0)
         rv(nc.scalar.copy, 1, NH, N)
@@ -358,26 +365,31 @@ def tile_gcam_pb_t_kernel(tc, attention, v, x, wf, b_fuse, gamma, out):
         nc.vector.tensor_copy(out=bias_f[:], in_=bias_b[:])
         alloc_xc(1)
         pxs(1)
-        qx(0, 0, NH)
-        m2(0, 0, NH)
-        qv(1, NH, N)
-        so(0, 0, NH)
         qx(0, NH, N)
         m2(0, NH, N)
+        qx(0, 0, NH)
+        m2(0, 0, NH)
+        so(0, 0, NH)
+        qv(1, NH, N)
 
         for i in range(1, B - 1):
             n = i + 1
+            zi = i % 2 == 0
+            zn = n % 2 == 0
+            if zi:
+                m1(i, 4)
             alloc_v(n)
             rv(nc.scalar.copy, n, 0, NH)
             so(i - 1, NH, N)
             store(i - 1, 0, N)
             alloc_z(i)
             alloc_xc(n)
-            tick_gx(i)
+            tick_gx(i, (lambda: za(i, 0)) if zi else None)
             for nb in range(8):
-                stt(i, nb)
-                if nb + 4 < 8:
-                    m1(i, nb + 4)
+                if not (zi and nb == 0):
+                    stt(i, nb)
+                    if nb + 4 < 8:
+                        m1(i, nb + 4)
             t_sa(n)
             load_att(n + RAW_BUFS, 1)
             px(n, 0)
@@ -386,7 +398,6 @@ def tile_gcam_pb_t_kernel(tc, attention, v, x, wf, b_fuse, gamma, out):
             load_v(n + RAW_BUFS, (0, N))
             sx(n, 0)
             sx(n, NQ)
-            load_x(i + RAW_BUFS, 0, N)
             qv(n, 0, NH)
             qx(i, 0, NH)
             qz(i, 0, NH)
@@ -396,6 +407,11 @@ def tile_gcam_pb_t_kernel(tc, attention, v, x, wf, b_fuse, gamma, out):
             qa(n, 0, C)
             for nb in range(4):
                 m1(n, nb)
+            if zn:
+                zs(n, 0)
+                px(n, 2 * NQ)
+                sx(n, 2 * NQ)
+            load_x(i + RAW_BUFS, 0, N)
             qz(i, NH, N)
             qx(i, NH, N)
             m2(i, NH, N)

@@ -109,11 +109,11 @@ def tile_gcam_pb_t_kernel(tc, attention, v, x, wf, b_fuse, gamma, out):
             s["xg"] = grp.tile([P, N, PACK], BF16, name="xg", tag="xg", align_bytes=64)
 
         def split(b):
-            return 712 if b in (2, 4, 6) else XS
+            return 640 if b in (2, 4, 6) else XS
 
         def px(b, h):
             s = st[b]
-            top = min(h + NQ, split(b))
+            top = min(h + NQ, XS)
             tp = ps_t.tile([P, NQ, PACK], BF16, name="tp", tag="tp")
             for lo in range(h, top, NB):
                 hi = min(lo + NB, top)
@@ -128,11 +128,14 @@ def tile_gcam_pb_t_kernel(tc, attention, v, x, wf, b_fuse, gamma, out):
 
         def sx(b, h):
             s = st[b]
-            top = min(h + NQ, split(b))
+            top = min(h + NQ, XS)
             nc.scalar.copy(
                 out=s["xg"][:, h:top, :].rearrange("p n t -> p (n t)").bitcast(F32),
                 in_=s["xp", h][:, 0 : top - h, :].rearrange("p n t -> p (n t)").bitcast(F32),
             )
+
+        def rx(b, lo, hi):
+            regroup(nc.scalar.copy, st[b]["xg"], st[b]["x_raw"], lo, hi, lo)
 
         def pxs(b):
             for h in range(0, XS, NQ):
@@ -167,7 +170,7 @@ def tile_gcam_pb_t_kernel(tc, attention, v, x, wf, b_fuse, gamma, out):
             s = st[b]
             tick = grp.tile([P, 1], F32, name="tick", tag="tick")
             nc.vector.memset(tick[:], 1.0)
-            gw = GW if split(b) == XS else 104
+            gw = GW if split(b) == XS else 128
             for lo in range(split(b), N, gw):
                 nc.gpsimd.tensor_scalar(
                     out=s["xg"][:, lo : lo + gw, :],
@@ -374,8 +377,8 @@ def tile_gcam_pb_t_kernel(tc, attention, v, x, wf, b_fuse, gamma, out):
 
         for i in range(1, B - 1):
             n = i + 1
-            zi = i % 2 == 0
-            zn = n % 2 == 0
+            zi = i in (2, 4, 6)
+            zn = n in (2, 4, 6)
             if zi:
                 m1(i, 4)
             alloc_v(n)
@@ -398,6 +401,8 @@ def tile_gcam_pb_t_kernel(tc, attention, v, x, wf, b_fuse, gamma, out):
             load_v(n + RAW_BUFS, (0, N))
             sx(n, 0)
             sx(n, NQ)
+            if zn:
+                rx(n, XS, split(n))
             qv(n, 0, NH)
             qx(i, 0, NH)
             qz(i, 0, NH)
@@ -409,8 +414,6 @@ def tile_gcam_pb_t_kernel(tc, attention, v, x, wf, b_fuse, gamma, out):
                 m1(n, nb)
             if zn:
                 zs(n, 0)
-                px(n, 2 * NQ)
-                sx(n, 2 * NQ)
             load_x(i + RAW_BUFS, 0, N)
             qz(i, NH, N)
             qx(i, NH, N)
@@ -424,28 +427,28 @@ def tile_gcam_pb_t_kernel(tc, attention, v, x, wf, b_fuse, gamma, out):
         m1(i, 5)
         so(i - 1, NH, N)
         store(i - 1, 0, N)
-        regroup(nc.scalar.copy, st[i]["xg"], st[i]["x_raw"], XS, N, XS)
         alloc_z(i)
         za(i, 0)
         za(i, 1)
+        rx(i, XS, N)
         for nb in range(2, 8):
             stt(i, nb)
             if nb + 4 < 8:
                 m1(i, nb + 4)
-        qx(i, NH, N)
-        m2x(i, NH, N, ps_a, "acc")
-        qz(i, NH, N)
-        m2z(i, NH, N)
-        so(i, NH, N)
-        store(i, NH, N)
         qx(i, 0, NH)
-        m2x(i, 0, NQ, ps_a, "acc")
-        m2x(i, NQ, NH, ps_a, "acc")
-        qz(i, 0, NQ)
-        m2z(i, 0, NQ)
-        so(i, 0, NQ)
-        store(i, 0, NQ)
-        qz(i, NQ, NH)
-        m2z(i, NQ, NH)
-        so(i, NQ, NH)
-        store(i, NQ, NH)
+        m2x(i, 0, NH, ps_a, "acc")
+        qz(i, 0, NH)
+        m2z(i, 0, NH)
+        so(i, 0, NH)
+        store(i, 0, NH)
+        qx(i, NH, N)
+        m2x(i, NH, NH + NQ, ps_a, "acc")
+        m2x(i, NH + NQ, N, ps_a, "acc")
+        qz(i, NH, NH + NQ)
+        m2z(i, NH, NH + NQ)
+        so(i, NH, NH + NQ)
+        store(i, NH, NH + NQ)
+        qz(i, NH + NQ, N)
+        m2z(i, NH + NQ, N)
+        so(i, NH + NQ, N)
+        store(i, NH + NQ, N)

@@ -66,14 +66,31 @@ def tile_gcam_pb_t_kernel(tc, attention, v, x, wf, b_fuse, gamma, out):
                 in_=tp[:].rearrange("p u c -> p c u"),
             )
 
+        def load_rows(dst, src, lo, hi, width):
+            if hi - lo == width:
+                nc.sync.dma_start(
+                    out=dst[:].rearrange("p (u e) n -> p u (e n)", u=2),
+                    in_=src.rearrange("(u p e) n -> p u (e n)", u=2, e=2),
+                )
+            else:
+                for u in range(2):
+                    nc.sync.dma_start(
+                        out=dst[:, 2 * u : 2 * u + 2, lo:hi],
+                        in_=src[2 * P * u : 2 * P * (u + 1), lo:hi].rearrange("(p e) n -> p e n", e=2),
+                    )
+
         def load_att(b, pieces):
             if b >= B:
                 return
             t = raw.tile([P, PACK, C], BF16, name="att_raw", tag="att_raw")
-            view = attention[b].rearrange("(p t) d -> p t d", t=PACK)
-            w = PACK // pieces
-            for k in range(pieces):
-                nc.sync.dma_start(out=t[:, k * w : (k + 1) * w, :], in_=view[:, k * w : (k + 1) * w, :])
+            if pieces == 1:
+                load_rows(t, attention[b], 0, C, C)
+            else:
+                for u in range(2):
+                    nc.sync.dma_start(
+                        out=t[:, 2 * u : 2 * u + 2, :],
+                        in_=attention[b][2 * P * u : 2 * P * (u + 1), :].rearrange("(p e) d -> p e d", e=2),
+                    )
             st[b]["att_raw"] = t
 
         def load_v(b, edges):
@@ -81,17 +98,15 @@ def tile_gcam_pb_t_kernel(tc, attention, v, x, wf, b_fuse, gamma, out):
                 return
             if "v_raw" not in st[b]:
                 st[b]["v_raw"] = raw.tile([P, PACK, N], BF16, name="v_raw", tag="v_raw")
-            view = v[b].rearrange("(p t) n -> p t n", t=PACK)
             for lo, hi in zip(edges, edges[1:]):
-                nc.sync.dma_start(out=st[b]["v_raw"][:, :, lo:hi], in_=view[:, :, lo:hi])
+                load_rows(st[b]["v_raw"], v[b], lo, hi, N)
 
         def load_x(b, lo, hi):
             if b >= B:
                 return
             if "x_raw" not in st[b]:
                 st[b]["x_raw"] = raw.tile([P, PACK, N], BF16, name="x_raw", tag="x_raw")
-            view = x[b].rearrange("(p t) n -> p t n", t=PACK)
-            nc.sync.dma_start(out=st[b]["x_raw"][:, :, lo:hi], in_=view[:, :, lo:hi])
+            load_rows(st[b]["x_raw"], x[b], lo, hi, N)
 
         def alloc_v(b):
             s = st[b]
@@ -107,9 +122,6 @@ def tile_gcam_pb_t_kernel(tc, attention, v, x, wf, b_fuse, gamma, out):
             s["x_codes"] = cod.tile([P, N], U32, name="x_codes", tag="x_codes", align_bytes=64)
             s["x_scales"] = cod.tile([P, N], U8, name="x_scales", tag="x_scales", align_bytes=64)
             s["xg"] = grp.tile([P, N, PACK], BF16, name="xg", tag="xg", align_bytes=64)
-
-        def split(b):
-            return 640 if b in (2, 4, 6) else XS
 
         def px(b, h):
             s = st[b]
@@ -138,14 +150,14 @@ def tile_gcam_pb_t_kernel(tc, attention, v, x, wf, b_fuse, gamma, out):
             regroup(nc.scalar.copy, st[b]["xg"], st[b]["x_raw"], lo, hi, lo)
 
         def pxs(b):
-            for h in range(0, XS, NQ):
-                px(b, h)
-                sx(b, h)
+            px(b, 0)
+            rx(b, NQ, XS)
+            sx(b, 0)
 
         def t_sa(b):
             s = st[b]
             s["attg"] = grp.tile([P, C, PACK], BF16, name="attg", tag="attg", align_bytes=64)
-            words = s["att_raw"][:].bitcast(F32).rearrange("p t (i u) -> p t u i", u=2)
+            words = s["att_raw"][:].bitcast(F32).rearrange("p t (u i) -> p t u i", u=2)
             for h in range(2):
                 transpose_words(words[:, 2 * h : 2 * h + 2, :, :], s["attg"][:].bitcast(F32), 256 * h)
 
@@ -170,17 +182,16 @@ def tile_gcam_pb_t_kernel(tc, attention, v, x, wf, b_fuse, gamma, out):
             s = st[b]
             tick = grp.tile([P, 1], F32, name="tick", tag="tick")
             nc.vector.memset(tick[:], 1.0)
-            gw = GW if split(b) == XS else 128
-            for lo in range(split(b), N, gw):
+            for lo in range(XS, N, GW):
                 nc.gpsimd.tensor_scalar(
-                    out=s["xg"][:, lo : lo + gw, :],
-                    in0=s["x_raw"][:, :, lo : lo + gw].rearrange("p t n -> p n t"),
+                    out=s["xg"][:, lo : lo + GW, :],
+                    in0=s["x_raw"][:, :, lo : lo + GW].rearrange("p t n -> p n t"),
                     scalar1=tick[:, 0:1],
                     scalar2=0.0,
                     op0=ALU.mult,
                     op1=ALU.add,
                 )
-                if lo == split(b) and then is not None:
+                if lo == XS and then is not None:
                     then()
 
         def alloc_z(b):
@@ -292,7 +303,7 @@ def tile_gcam_pb_t_kernel(tc, attention, v, x, wf, b_fuse, gamma, out):
         nc.sync.dma_start(out=gamma_b[:], in_=gamma.partition_broadcast(P))
         wf_raw = consts.tile([P, 2 * C], BF16, name="wf_raw")
         nc.sync.dma_start(out=wf_raw[:], in_=wf)
-        load_v(1, (0, NH, N))
+        load_v(1, (0, N))
         load_x(0, XS, N)
         load_att(1, 1)
         load_x(0, 0, XS)
@@ -340,7 +351,7 @@ def tile_gcam_pb_t_kernel(tc, attention, v, x, wf, b_fuse, gamma, out):
         wf_codes = consts.tile([P, 2 * O], U32, name="wf_codes", align_bytes=64)
         wf_scales = consts.tile([P, 2 * O], U8, name="wf_scales", align_bytes=64)
         transpose_words(
-            wf_raw[:].bitcast(F32).rearrange("p (g i u) -> p g u i", g=2, u=2),
+            wf_raw[:].bitcast(F32).rearrange("p (g u i) -> p g u i", g=2, u=2),
             wfg[:].bitcast(F32),
             0,
         )
@@ -377,32 +388,25 @@ def tile_gcam_pb_t_kernel(tc, attention, v, x, wf, b_fuse, gamma, out):
 
         for i in range(1, B - 1):
             n = i + 1
-            zi = i in (2, 4, 6)
-            zn = n in (2, 4, 6)
-            if zi:
-                m1(i, 4)
             alloc_v(n)
             rv(nc.scalar.copy, n, 0, NH)
             so(i - 1, NH, N)
             store(i - 1, 0, N)
             alloc_z(i)
             alloc_xc(n)
-            tick_gx(i, (lambda: za(i, 0)) if zi else None)
+            tick_gx(i)
             for nb in range(8):
-                if not (zi and nb == 0):
-                    stt(i, nb)
-                    if nb + 4 < 8:
-                        m1(i, nb + 4)
+                stt(i, nb)
+                if nb + 4 < 8:
+                    m1(i, nb + 4)
             t_sa(n)
             load_att(n + RAW_BUFS, 1)
             px(n, 0)
-            px(n, NQ)
             rv(nc.scalar.copy, n, NH, N)
             load_v(n + RAW_BUFS, (0, N))
+            rx(n, NQ, XS)
             sx(n, 0)
-            sx(n, NQ)
-            if zn:
-                rx(n, XS, split(n))
+            load_x(i + RAW_BUFS, 0, N)
             qv(n, 0, NH)
             qx(i, 0, NH)
             qz(i, 0, NH)
@@ -412,9 +416,6 @@ def tile_gcam_pb_t_kernel(tc, attention, v, x, wf, b_fuse, gamma, out):
             qa(n, 0, C)
             for nb in range(4):
                 m1(n, nb)
-            if zn:
-                zs(n, 0)
-            load_x(i + RAW_BUFS, 0, N)
             qz(i, NH, N)
             qx(i, NH, N)
             m2(i, NH, N)

@@ -19,7 +19,7 @@ NH = 512
 NQ = 256
 XG = 512
 XS = N - XG
-GW = 128
+ZI = (2, 4, 6)
 RAW_BUFS = 4
 FLOPS = 2 * B * C * C * N + 2 * B * O * 2 * C * N
 
@@ -123,6 +123,9 @@ def tile_gcam_pb_t_kernel(tc, attention, v, x, wf, b_fuse, gamma, out):
             s["x_scales"] = cod.tile([P, N], U8, name="x_scales", tag="x_scales", align_bytes=64)
             s["xg"] = grp.tile([P, N, PACK], BF16, name="xg", tag="xg", align_bytes=64)
 
+        def split(b):
+            return N - 384 if b in ZI else XS
+
         def px(b, h):
             s = st[b]
             top = min(h + NQ, XS)
@@ -182,17 +185,17 @@ def tile_gcam_pb_t_kernel(tc, attention, v, x, wf, b_fuse, gamma, out):
             s = st[b]
             tick = grp.tile([P, 1], F32, name="tick", tag="tick")
             nc.vector.memset(tick[:], 1.0)
-            for lo in range(XS, N, GW):
-                nc.gpsimd.tensor_scalar(
-                    out=s["xg"][:, lo : lo + GW, :],
-                    in0=s["x_raw"][:, :, lo : lo + GW].rearrange("p t n -> p n t"),
-                    scalar1=tick[:, 0:1],
-                    scalar2=0.0,
-                    op0=ALU.mult,
-                    op1=ALU.add,
-                )
-                if lo == XS and then is not None:
-                    then()
+            lo = split(b)
+            nc.gpsimd.tensor_scalar(
+                out=s["xg"][:, lo:N, :],
+                in0=s["x_raw"][:, :, lo:N].rearrange("p t n -> p n t"),
+                scalar1=tick[:, 0:1],
+                scalar2=0.0,
+                op0=ALU.mult,
+                op1=ALU.add,
+            )
+            if then is not None:
+                then()
 
         def alloc_z(b):
             s = st[b]
@@ -388,27 +391,35 @@ def tile_gcam_pb_t_kernel(tc, attention, v, x, wf, b_fuse, gamma, out):
 
         for i in range(1, B - 1):
             n = i + 1
+            zi = i in ZI
+            zn = n in ZI
+            if zi:
+                m1(i, 4)
             alloc_v(n)
             rv(nc.scalar.copy, n, 0, NH)
             so(i - 1, NH, N)
             store(i - 1, 0, N)
             alloc_z(i)
             alloc_xc(n)
-            tick_gx(i)
+            tick_gx(i, (lambda: za(i, 0)) if zi else None)
             for nb in range(8):
-                stt(i, nb)
-                if nb + 4 < 8:
-                    m1(i, nb + 4)
+                if not (zi and nb == 0):
+                    stt(i, nb)
+                    if nb + 4 < 8:
+                        m1(i, nb + 4)
             t_sa(n)
             load_att(n + RAW_BUFS, 1)
             px(n, 0)
+            px(n, NQ)
             rv(nc.scalar.copy, n, NH, N)
             load_v(n + RAW_BUFS, (0, N))
-            rx(n, NQ, XS)
             sx(n, 0)
+            sx(n, NQ)
+            if zn:
+                rx(n, XS, split(n))
             load_x(i + RAW_BUFS, 0, N)
             qv(n, 0, NH)
-            qx(i, 0, NH)
+            qx(i, 0, N)
             qz(i, 0, NH)
             m2(i, 0, NH)
             so(i, 0, NH)
@@ -416,8 +427,9 @@ def tile_gcam_pb_t_kernel(tc, attention, v, x, wf, b_fuse, gamma, out):
             qa(n, 0, C)
             for nb in range(4):
                 m1(n, nb)
+            if zn:
+                zs(n, 0)
             qz(i, NH, N)
-            qx(i, NH, N)
             m2(i, NH, N)
             qv(n, NH, N)
 

from contextlib import ExitStack

import concourse.mybir as mybir
from concourse.masks import make_identity

BF16 = mybir.dt.bfloat16
F32 = mybir.dt.float32
U32 = mybir.dt.uint32
U8 = mybir.dt.uint8
FP8X4 = mybir.dt.float8_e4m3fn_x4
ALU = mybir.AluOpType
ACT = mybir.ActivationFunctionType

B, C, N, O = 8, 512, 1024, 128
P = 128
PACK = 4
NB = 128
NH = 512
NQ = 256
XG = 512
XS = N - XG
ZI = (2, 4, 6)
RAW_BUFS = 4
FLOPS = 2 * B * C * C * N + 2 * B * O * 2 * C * N


def tile_gcam_pb_t_kernel(tc, attention, v, x, wf, b_fuse, gamma, out):
    nc = tc.nc
    with ExitStack() as ctx:
        consts = ctx.enter_context(tc.tile_pool(name="consts", bufs=1))
        raw = ctx.enter_context(tc.tile_pool(name="raw", bufs=RAW_BUFS))
        grp = ctx.enter_context(tc.tile_pool(name="grp", bufs=2))
        cod = ctx.enter_context(tc.tile_pool(name="cod", bufs=2))
        res = ctx.enter_context(tc.tile_pool(name="res", bufs=4))
        ps_t = ctx.enter_context(tc.psum_pool(name="ps_t", bufs=2))
        ps_a = ctx.enter_context(tc.psum_pool(name="ps_a", bufs=4))
        ps_o = ctx.enter_context(tc.psum_pool(name="ps_o", bufs=2))
        ctx.enter_context(tc.manual_schedule())

        st = {}
        for b in range(B):
            st[b] = {}

        def regroup(engine_copy, dst, src, lo, hi, dst_lo):
            engine_copy(
                out=dst[:, dst_lo : dst_lo + hi - lo, :].rearrange("p (c i) t -> p c t i", i=4),
                in_=src[:, :, lo:hi].rearrange("p t (c i) -> p c t i", i=4),
            )

        def quantise(codes, scales, grouped, lo, hi, src_lo):
            nc.vector.quantize_mx(
                out=codes[:, lo:hi].bitcast(FP8X4),
                scales=scales[:, lo:hi],
                in_=grouped[:, src_lo : src_lo + hi - lo, :].rearrange("p n t -> p (n t)"),
            )

        def transpose_words(words, dst_words, col0):
            tp = ps_t.tile([P, 2, 256], F32, name="tp", tag="tp")
            for blk in range(2):
                for u in range(2):
                    nc.tensor.transpose(
                        tp[:, u, blk * P : (blk + 1) * P], words[:, blk, u, :], ident[:]
                    )
            nc.scalar.copy(
                out=dst_words[:, col0 : col0 + 256, :],
                in_=tp[:].rearrange("p u c -> p c u"),
            )

        def load_rows(dst, src, lo, hi, width):
            if hi - lo == width:
                nc.sync.dma_start(
                    out=dst[:].rearrange("p (u e) n -> p u (e n)", u=2),
                    in_=src.rearrange("(u p e) n -> p u (e n)", u=2, e=2),
                )
            else:
                for u in range(2):
                    nc.sync.dma_start(
                        out=dst[:, 2 * u : 2 * u + 2, lo:hi],
                        in_=src[2 * P * u : 2 * P * (u + 1), lo:hi].rearrange("(p e) n -> p e n", e=2),
                    )

        def load_att(b, pieces):
            if b >= B:
                return
            t = raw.tile([P, PACK, C], BF16, name="att_raw", tag="att_raw")
            if pieces == 1:
                load_rows(t, attention[b], 0, C, C)
            else:
                for u in range(2):
                    nc.sync.dma_start(
                        out=t[:, 2 * u : 2 * u + 2, :],
                        in_=attention[b][2 * P * u : 2 * P * (u + 1), :].rearrange("(p e) d -> p e d", e=2),
                    )
            st[b]["att_raw"] = t

        def load_v(b, edges):
            if b >= B:
                return
            if "v_raw" not in st[b]:
                st[b]["v_raw"] = raw.tile([P, PACK, N], BF16, name="v_raw", tag="v_raw")
            for lo, hi in zip(edges, edges[1:]):
                load_rows(st[b]["v_raw"], v[b], lo, hi, N)

        def load_x(b, lo, hi):
            if b >= B:
                return
            if "x_raw" not in st[b]:
                st[b]["x_raw"] = raw.tile([P, PACK, N], BF16, name="x_raw", tag="x_raw")
            load_rows(st[b]["x_raw"], x[b], lo, hi, N)

        def alloc_v(b):
            s = st[b]
            s["vg"] = grp.tile([P, N, PACK], BF16, name="vg", tag="vg", align_bytes=64)
            s["v_codes"] = cod.tile([P, N], U32, name="v_codes", tag="v_codes", align_bytes=64)
            s["v_scales"] = cod.tile([P, N], U8, name="v_scales", tag="v_scales", align_bytes=64)

        def rv(engine_copy, b, lo, hi):
            regroup(engine_copy, st[b]["vg"], st[b]["v_raw"], lo, hi, lo)

        def alloc_xc(b):
            s = st[b]
            s["x_codes"] = cod.tile([P, N], U32, name="x_codes", tag="x_codes", align_bytes=64)
            s["x_scales"] = cod.tile([P, N], U8, name="x_scales", tag="x_scales", align_bytes=64)
            s["xg"] = grp.tile([P, N, PACK], BF16, name="xg", tag="xg", align_bytes=64)

        def split(b):
            return N - 384 if b in ZI else XS

        def px(b, h):
            s = st[b]
            top = min(h + NQ, XS)
            tp = ps_t.tile([P, NQ, PACK], BF16, name="tp", tag="tp")
            for lo in range(h, top, NB):
                hi = min(lo + NB, top)
                nc.tensor.matmul(
                    tp[:, lo - h : hi - h, :].rearrange("p n t -> p t n"),
                    lhsT=ident_b[:],
                    rhs=s["x_raw"][:, :, lo:hi],
                    start=True,
                    stop=True,
                )
            s["xp", h] = tp

        def sx(b, h):
            s = st[b]
            top = min(h + NQ, XS)
            nc.scalar.copy(
                out=s["xg"][:, h:top, :].rearrange("p n t -> p (n t)").bitcast(F32),
                in_=s["xp", h][:, 0 : top - h, :].rearrange("p n t -> p (n t)").bitcast(F32),
            )

        def rx(b, lo, hi):
            regroup(nc.scalar.copy, st[b]["xg"], st[b]["x_raw"], lo, hi, lo)

        def pxs(b):
            px(b, 0)
            rx(b, NQ, XS)
            sx(b, 0)

        def t_sa(b):
            s = st[b]
            s["attg"] = grp.tile([P, C, PACK], BF16, name="attg", tag="attg", align_bytes=64)
            words = s["att_raw"][:].bitcast(F32).rearrange("p t (u i) -> p t u i", u=2)
            for h in range(2):
                transpose_words(words[:, 2 * h : 2 * h + 2, :, :], s["attg"][:].bitcast(F32), 256 * h)

        def alloc_ac(b):
            s = st[b]
            s["att_codes"] = cod.tile([P, C], U32, name="att_codes", tag="att_codes", align_bytes=64)
            s["att_scales"] = cod.tile([P, C], U8, name="att_scales", tag="att_scales", align_bytes=64)

        def qa(b, lo, hi):
            s = st[b]
            quantise(s["att_codes"], s["att_scales"], s["attg"], lo, hi, lo)

        def qv(b, lo, hi):
            s = st[b]
            quantise(s["v_codes"], s["v_scales"], s["vg"], lo, hi, lo)

        def qx(b, lo, hi):
            s = st[b]
            quantise(s["x_codes"], s["x_scales"], s["xg"], lo, hi, lo)

        def tick_gx(b, then=None):
            s = st[b]
            tick = grp.tile([P, 1], F32, name="tick", tag="tick")
            nc.vector.memset(tick[:], 1.0)
            lo = split(b)
            nc.gpsimd.tensor_scalar(
                out=s["xg"][:, lo:N, :],
                in0=s["x_raw"][:, :, lo:N].rearrange("p t n -> p n t"),
                scalar1=tick[:, 0:1],
                scalar2=0.0,
                op0=ALU.mult,
                op1=ALU.add,
            )
            if then is not None:
                then()

        def alloc_z(b):
            s = st[b]
            s["zg"] = grp.tile([P, N, PACK], BF16, name="zg", tag="zg", align_bytes=64)
            s["z_codes"] = cod.tile([P, N], U32, name="z_codes", tag="z_codes", align_bytes=64)
            s["z_scales"] = cod.tile([P, N], U8, name="z_scales", tag="z_scales", align_bytes=64)

        def m1(b, nb):
            s = st[b]
            cols = slice(nb * NB, (nb + 1) * NB)
            acc = ps_a.tile([P, PACK, NB], F32, name="acc", tag="acc")
            for t in range(PACK):
                rows = slice(t * P, (t + 1) * P)
                nc.tensor.matmul_mx(
                    out=acc[:, t, :],
                    lhsT=s["att_codes"][:, rows].bitcast(FP8X4),
                    lhsT_scale=s["att_scales"][:, rows],
                    rhs=s["v_codes"][:, cols].bitcast(FP8X4),
                    rhs_scale=s["v_scales"][:, cols],
                    start=True,
                    stop=True,
                )
            s["acc", nb] = acc

        def stt(b, nb):
            s = st[b]
            cols = slice(nb * NB, (nb + 1) * NB)
            nc.vector.scalar_tensor_tensor(
                out=s["zg"][:, cols, :],
                in0=s["acc", nb][:].rearrange("p t n -> p n t"),
                scalar=gamma_f[:, 0:1],
                in1=s["vg"][:, cols, :],
                op0=ALU.mult,
                op1=ALU.add,
            )

        def zs(b, nb):
            s = st[b]
            zt = grp.tile([P, NB, PACK], F32, name="zt", tag="zt")
            s["zt", nb] = zt
            nc.scalar.activation(
                out=zt[:], in_=s["acc", nb][:].rearrange("p t n -> p n t"), func=ACT.Copy,
                scale=gamma_f[:, 0:1],
            )

        def za(b, nb):
            s = st[b]
            cols = slice(nb * NB, (nb + 1) * NB)
            nc.gpsimd.tensor_tensor(
                out=s["zg"][:, cols, :], in0=s["zt", nb][:], in1=s["vg"][:, cols, :], op=ALU.add
            )

        def qz(b, lo, hi):
            s = st[b]
            quantise(s["z_codes"], s["z_scales"], s["zg"], lo, hi, lo)

        def m2x(b, lo, hi, pool, tag):
            s = st[b]
            cols = slice(lo, hi)
            acc2 = pool.tile([P, NH], F32, name="acc2", tag=tag)
            nc.tensor.matmul_mx(
                out=acc2[:, 0 : hi - lo],
                lhsT=wf_codes[:, P : 2 * P].bitcast(FP8X4),
                lhsT_scale=wf_scales[:, P : 2 * P],
                rhs=s["x_codes"][:, cols].bitcast(FP8X4),
                rhs_scale=s["x_scales"][:, cols],
                start=True,
                stop=False,
            )
            s["acc2", lo] = acc2

        def m2z(b, lo, hi):
            s = st[b]
            cols = slice(lo, hi)
            nc.tensor.matmul_mx(
                out=s["acc2", lo][:, 0 : hi - lo],
                lhsT=wf_codes[:, 0:P].bitcast(FP8X4),
                lhsT_scale=wf_scales[:, 0:P],
                rhs=s["z_codes"][:, cols].bitcast(FP8X4),
                rhs_scale=s["z_scales"][:, cols],
                start=False,
                stop=True,
            )

        def m2(b, lo, hi):
            m2x(b, lo, hi, ps_o, "acc2")
            m2z(b, lo, hi)

        def so(b, lo, hi):
            s = st[b]
            if "out_sb" not in s:
                s["out_sb"] = res.tile([P, N], F32, name="out_sb", tag="out_sb")
            nc.scalar.activation(
                out=s["out_sb"][:, lo:hi], in_=s["acc2", lo][:, 0 : hi - lo], func=ACT.Identity,
                bias=bias_f[:, 0:1], scale=1.0,
            )

        def store(b, lo, hi):
            nc.sync.dma_start(out=out[b][:, lo:hi], in_=st[b]["out_sb"][:, lo:hi])

        ident = consts.tile([P, P], F32, name="ident")
        make_identity(nc, ident[:])
        ident_b = consts.tile([P, P], BF16, name="ident_b")
        make_identity(nc, ident_b[:])
        load_att(0, 2)
        load_v(0, (0, NQ, NH, NH + NQ, N))
        gamma_b = consts.tile([P, 1], BF16, name="gamma_b")
        nc.sync.dma_start(out=gamma_b[:], in_=gamma.partition_broadcast(P))
        wf_raw = consts.tile([P, 2 * C], BF16, name="wf_raw")
        nc.sync.dma_start(out=wf_raw[:], in_=wf)
        load_v(1, (0, N))
        load_x(0, XS, N)
        load_att(1, 1)
        load_x(0, 0, XS)
        load_x(1, 0, N)
        bias_b = consts.tile([P, 1], BF16, name="bias_b")
        with nc.allow_non_contiguous_dma(reason="one bias value a partition, 128 in all"):
            nc.sync.dma_start(out=bias_b[:], in_=b_fuse.rearrange("(o one) -> o one", one=1))
        for b in range(2, RAW_BUFS):
            load_v(b, (0, N))
            load_att(b, 1)
            load_x(b, 0, N)

        t_sa(0)
        load_att(RAW_BUFS, 1)
        alloc_v(0)
        alloc_ac(0)
        rv(nc.vector.tensor_copy, 0, 0, NQ)
        rv(nc.vector.tensor_copy, 0, NQ, NH)
        qv(0, 0, NQ)
        qa(0, 0, NQ)
        qa(0, NQ, C)
        qv(0, NQ, NH)
        rv(nc.scalar.copy, 0, NH, NH + NQ)
        rv(nc.scalar.copy, 0, NH + NQ, N)
        load_v(RAW_BUFS, (0, N))
        m1(0, 0)
        m1(0, 1)
        m1(0, 2)
        m1(0, 3)
        gamma_f = consts.tile([P, 1], F32, name="gamma_f")
        nc.vector.tensor_copy(out=gamma_f[:], in_=gamma_b[:])
        bias_f = consts.tile([P, 1], F32, name="bias_f")

        alloc_z(0)
        alloc_xc(0)
        qv(0, NH, NH + NQ)
        tick_gx(0)
        stt(0, 0)
        m1(0, 4)
        stt(0, 1)
        m1(0, 5)
        alloc_v(1)
        rv(nc.scalar.copy, 1, 0, NH)
        wfg = consts.tile([P, 2 * O, PACK], BF16, name="wfg", align_bytes=64)
        wf_codes = consts.tile([P, 2 * O], U32, name="wf_codes", align_bytes=64)
        wf_scales = consts.tile([P, 2 * O], U8, name="wf_scales", align_bytes=64)
        transpose_words(
            wf_raw[:].bitcast(F32).rearrange("p (g u i) -> p g u i", g=2, u=2),
            wfg[:].bitcast(F32),
            0,
        )
        stt(0, 2)
        qv(0, NH + NQ, N)
        m1(0, 6)
        stt(0, 3)
        m1(0, 7)
        t_sa(1)
        load_att(1 + RAW_BUFS, 1)
        for nb in range(4, 8):
            stt(0, nb)
        pxs(0)
        rv(nc.scalar.copy, 1, NH, N)
        load_v(1 + RAW_BUFS, (0, N))
        load_x(RAW_BUFS, 0, N)
        quantise(wf_codes, wf_scales, wfg, 0, 2 * O, 0)
        qv(1, 0, NH)
        alloc_ac(1)
        qa(1, 0, C)
        for nb in range(4):
            m1(1, nb)
        qz(0, 0, NH)
        qz(0, NH, N)
        nc.vector.tensor_copy(out=bias_f[:], in_=bias_b[:])
        alloc_xc(1)
        pxs(1)
        qx(0, NH, N)
        m2(0, NH, N)
        qx(0, 0, NH)
        m2(0, 0, NH)
        so(0, 0, NH)
        qv(1, NH, N)

        for i in range(1, B - 1):
            n = i + 1
            zi = i in ZI
            zn = n in ZI
            if zi:
                m1(i, 4)
            alloc_v(n)
            rv(nc.scalar.copy, n, 0, NH)
            so(i - 1, NH, N)
            store(i - 1, 0, N)
            alloc_z(i)
            alloc_xc(n)
            tick_gx(i, (lambda: za(i, 0)) if zi else None)
            for nb in range(8):
                if not (zi and nb == 0):
                    stt(i, nb)
                    if nb + 4 < 8:
                        m1(i, nb + 4)
            t_sa(n)
            load_att(n + RAW_BUFS, 1)
            px(n, 0)
            px(n, NQ)
            rv(nc.scalar.copy, n, NH, N)
            load_v(n + RAW_BUFS, (0, N))
            sx(n, 0)
            sx(n, NQ)
            if zn:
                rx(n, XS, split(n))
            load_x(i + RAW_BUFS, 0, N)
            qv(n, 0, NH)
            qx(i, 0, N)
            qz(i, 0, NH)
            m2(i, 0, NH)
            so(i, 0, NH)
            alloc_ac(n)
            qa(n, 0, C)
            for nb in range(4):
                m1(n, nb)
            if zn:
                zs(n, 0)
            qz(i, NH, N)
            m2(i, NH, N)
            qv(n, NH, N)

        i = B - 1
        zs(i, 0)
        m1(i, 4)
        zs(i, 1)
        m1(i, 5)
        so(i - 1, NH, N)
        store(i - 1, 0, N)
        alloc_z(i)
        za(i, 0)
        za(i, 1)
        rx(i, XS, N)
        for nb in range(2, 8):
            stt(i, nb)
            if nb + 4 < 8:
                m1(i, nb + 4)
        qx(i, 0, NH)
        m2x(i, 0, NH, ps_a, "acc")
        qz(i, 0, NH)
        m2z(i, 0, NH)
        so(i, 0, NH)
        store(i, 0, NH)
        qx(i, NH, N)
        m2x(i, NH, NH + NQ, ps_a, "acc")
        m2x(i, NH + NQ, N, ps_a, "acc")
        qz(i, NH, NH + NQ)
        m2z(i, NH, NH + NQ)
        so(i, NH, NH + NQ)
        store(i, NH, NH + NQ)
        qz(i, NH + NQ, N)
        m2z(i, NH + NQ, N)
        so(i, NH + NQ, N)
        store(i, NH + NQ, N)
